import numpy as np
import ml_dtypes


def mxq(x, axis, fmt="e4m3"):
    dtype, down = {"e4m3": (ml_dtypes.float8_e4m3fn, 7), "e5m2": (ml_dtypes.float8_e5m2, 14)}[fmt]
    v = np.moveaxis(np.asarray(x, np.float32).astype(ml_dtypes.bfloat16).astype(np.float64), axis, -1)
    blocks = v.reshape(v.shape[:-1] + (-1, 32))
    amax = np.abs(blocks).max(-1, keepdims=True)
    byte = np.maximum(np.where(amax > 0, np.frexp(amax)[1] - 1 + 127, 0) - down, 1)
    scale = np.exp2(byte - 127.0)
    codes = (blocks / scale).astype(np.float32).astype(dtype).astype(np.float64)
    return np.moveaxis((codes * scale).reshape(v.shape), -1, axis)


WIDE = False


def mx_kscale(k):
    if not WIDE:
        return np.ones(k)
    levels = np.array([10, -10, 5, -5, 0])
    if k % 512:
        return np.exp2(np.random.permutation(np.resize(levels, k // 32))).repeat(32)
    a = np.empty((k // 512, 16))
    for p in range(k // 512):
        a[p, :8] = np.random.permutation(np.resize(levels, 8))
        for g in range(8):
            far = levels[np.abs(levels - a[p, g]) >= 10]
            a[p, g + 8] = far[np.random.randint(len(far))]
    return np.exp2(a.ravel()).repeat(32)


BF16 = ml_dtypes.bfloat16


def bf(x):
    return np.asarray(x, np.float32).astype(BF16)


def f64(x):
    return np.asarray(x).astype(np.float64)


B, D_IN, H1, H2, H3, C = 8192, 2048, 2048, 2048, 1024, 512
BN_EPS = 1e-5


def bn_relu(z, gamma, beta):
    m = z.mean(axis=0)
    v = z.var(axis=0)
    return np.maximum((z - m) * (1.0 / np.sqrt(v + BN_EPS)) * gamma + beta, 0.0)


def setup_inputs():
    t = mx_kscale(H3)
    c = 32.0 * np.exp2(-15.0 * np.random.random(H3))
    mu = 0.5 * np.random.standard_normal(H3)
    return {"z2": bf((np.random.standard_normal((B, H3)) + mu) * c),
            "g2": bf((1.0 + 0.1 * np.random.standard_normal(H3)) * t),
            "beta2": bf(0.2 * np.random.standard_normal(H3) * t),
            "W3": bf(np.random.standard_normal((C, H3)) * 3.0 / np.sqrt(H3) / t),
            "b3": bf(0.5 * np.random.standard_normal(C))}


def reference(z2, g2, beta2, W3, b3):
    h = bn_relu(f64(z2), f64(g2), f64(beta2))
    logits = (mxq(h, 1, "e4m3") @ mxq(f64(W3), 1, "e4m3").T) + f64(b3)
    s = logits - logits.max(axis=1, keepdims=True)
    return s - np.log(np.exp(s).sum(axis=1, keepdims=True))

@@ -1,0 +1,476 @@
+from contextlib import ExitStack
+
+import concourse.mybir as mybir
+from concourse.masks import make_identity
+
+F32 = mybir.dt.float32
+BF16 = mybir.dt.bfloat16
+U32 = mybir.dt.uint32
+U8 = mybir.dt.uint8
+I32 = mybir.dt.int32
+FP8X4 = mybir.dt.float8_e4m3fn_x4
+ALU = mybir.AluOpType
+ACT = mybir.ActivationFunctionType
+AX = mybir.AxisListType
+
+P = 128
+B = 8192
+K = 1024
+C = 512
+KT = K // P
+PASS_K = 4 * P
+G = 8
+GB = B // G
+U = 16
+UB = B // U
+JH = UB // P
+J = GB // P
+NG = 3
+KS = KT - NG
+BN_EPS = 1e-5
+ROOT = 1024.0
+N_WARM = 12
+R_V_COLS = 128
+G_W = 1
+W_EARLY = 2
+GRAM_RUN = 4
+
+FLOPS = 2 * B * K * C
+
+
+def tile_cols(kt):
+    c, t = divmod(kt, 4)
+    return slice(c * PASS_K + t, (c + 1) * PASS_K, 4)
+
+
+def tile_binarymlp_pb_t_kernel(tc, z2, g2, beta2, W3, b3, out):
+    nc = tc.nc
+    with ExitStack() as ctx:
+        const = ctx.enter_context(tc.tile_pool(name="const", bufs=1))
+        big = ctx.enter_context(tc.tile_pool(name="big", bufs=11))
+        grp = ctx.enter_context(tc.tile_pool(name="grp", bufs=2))
+        cod = ctx.enter_context(tc.tile_pool(name="cod", bufs=4))
+        small = ctx.enter_context(tc.tile_pool(name="small", bufs=4))
+        psum = ctx.enter_context(tc.psum_pool(name="psum", bufs=8))
+        ctx.enter_context(tc.manual_schedule())
+
+        brow = const.tile([P, C], BF16, name="brow")
+        nc.vector.memset(brow[:], 0.0)
+        vecs = const.tile([P, PASS_K], BF16, name="vecs")
+        nc.vector.memset(vecs[:], 0.0)
+        nc.sync.dma_start(out=brow[0:1, :], in_=b3.rearrange("(o c) -> o c", o=1))
+        nc.sync.dma_start(out=vecs[0:2, :], in_=g2.rearrange("(c x) -> c x", x=PASS_K))
+        nc.sync.dma_start(out=vecs[2:4, :], in_=beta2.rearrange("(c x) -> c x", x=PASS_K))
+        wcodes = const.tile([P, 2 * C], U32, name="wcodes", align_bytes=64)
+        wscl = const.tile([P, 2 * C], U8, name="wscl", align_bytes=64)
+        nc.vector.memset(wcodes[:, 0:C].bitcast(I32), 0)
+        nc.vector.memset(wscl[:, 0:C].bitcast(I32), 0)
+        one = const.tile([P, 1], F32, name="one")
+        nc.vector.memset(one[:], 1.0)
+        warm = const.tile([P, 1], F32, name="warm")
+        nc.scalar.activation(out=warm[:], in_=one[:], func=ACT.Sqrt)
+
+        pwarm = psum.tile([P, C], F32, tag="ps", name="pwarm")
+        for i in range(N_WARM):
+            nc.tensor.matmul_mx(
+                out=pwarm[:],
+                lhsT=wcodes[:, 0:P].bitcast(FP8X4),
+                lhsT_scale=wscl[:, 0:P],
+                rhs=wcodes[:, 0:C].bitcast(FP8X4),
+                rhs_scale=wscl[:, 0:C],
+                start=True,
+                stop=True,
+            )
+
+        ident = const.tile([P, P], BF16, name="ident")
+        make_identity(nc, ident[:])
+        ones = const.tile([P, P], BF16, name="ones")
+        nc.vector.memset(ones[:], 1.0)
+        pe_pos = const.tile([P, J], F32, name="pe_pos")
+        nc.gpsimd.memset(pe_pos[:], 1.0 / ROOT)
+        pe_neg = const.tile([P, J], F32, name="pe_neg")
+        nc.gpsimd.memset(pe_neg[:], -1.0 / ROOT)
+
+        s1 = const.tile([P, KT, G], F32, name="s1")
+        sq = const.tile([P, KS, G], F32, name="sq")
+        nc.vector.memset(sq[:], 0.0)
+        sqv = const.tile([P, G // 2], F32, name="sqv")
+        junk_v = const.tile([P, GB], BF16, name="junk_v")
+        ssq = const.tile([P, KT], F32, name="ssq")
+        junk_s = const.tile([P, GB], BF16, name="junk_s")
+        junk_e = const.tile([P, C], BF16, name="junk_e")
+        junk_d = const.tile([P, P], F32, name="junk_d")
+        gb = const.tile([P, 2 * KT], F32, name="gb")
+        bias_bc = const.tile([P, C], F32, name="bias_bc")
+        grams = []
+        for i in range(NG):
+            grams.append(psum.tile([P, P], F32, tag="ps", name="gram%d" % i))
+
+        pv = psum.tile([P, 4, P], BF16, tag="ps", name="pv")
+        for t in range(4):
+            nc.tensor.transpose(pv[:, t, :], vecs[:, t:PASS_K:4], ident[:])
+        nc.vector.tensor_copy(
+            out=gb[:].rearrange("p (r t) -> p r t", t=4), in_=pv[:, :, 0:4].rearrange("p t r -> p r t")
+        )
+        pb = psum.tile([P, C], F32, tag="ps", name="pb")
+        nc.tensor.matmul(out=pb[:], lhsT=ones[:], rhs=brow[:], start=True, stop=True)
+        nc.scalar.copy(out=bias_bc[:], in_=pb[:])
+
+        zts = []
+        gram_jobs = [(i, j) for i in range(NG) for j in range(J)]
+        for g in range(G):
+            zt = big.tile([P, KT, GB], BF16, tag="big", name="zt%d" % g, align_bytes=64)
+            zts.append(zt)
+            zn = big.tile([P, J, K], BF16, tag="big", name="zn", align_bytes=64)
+            pieces = 2 if g == 0 else 1
+            for piece in range(pieces):
+                cols = slice(piece * K // pieces, (piece + 1) * K // pieces)
+                for h in range(2):
+                    u = 2 * g + h
+                    nc.sync.dma_start(
+                        out=zn[:, h * JH : (h + 1) * JH, cols],
+                        in_=z2[u * UB : (u + 1) * UB, cols].rearrange("(p j) k -> p j k", j=JH),
+                    )
+            if g == G_W:
+                wn = big.tile([P, C // P, K], BF16, tag="big", name="wn", align_bytes=64)
+                nc.sync.dma_start(out=wn[:], in_=W3.rearrange("(t p) k -> p t k", p=P))
+            for kt in range(KT):
+                ks = tile_cols(kt)
+                pt = psum.tile([P, GB], BF16, tag="ps", name="pt")
+                for j in range(J):
+                    nc.tensor.transpose(pt[:, j * P : (j + 1) * P], zn[:, j, ks], ident[:])
+                for i, j in gram_jobs[GRAM_RUN * kt : GRAM_RUN * (kt + 1)]:
+                    gs = tile_cols(KS + i)
+                    nc.tensor.matmul(
+                        out=grams[i][:],
+                        lhsT=zn[:, j, gs],
+                        rhs=zn[:, j, gs],
+                        start=(g == 0 and j == 0),
+                        stop=(g == G - 1 and j == J - 1),
+                    )
+                nc.vector.tensor_scalar(
+                    out=zt[:, kt, :],
+                    in0=pt[:],
+                    scalar1=1.0,
+                    scalar2=None,
+                    op0=ALU.mult,
+                    op1=ALU.add,
+                    accum_out=s1[:, kt, g : g + 1],
+                )
+                if kt < KS - 1 or (kt == KS - 1 and g % 2 == 0):
+                    nc.scalar.activation(
+                        out=junk_s[:],
+                        in_=zt[:, kt, :],
+                        func=ACT.Square,
+                        accum_out=sq[:, kt, g : g + 1],
+                    )
+                if kt == KS and g % 2 == 1:
+                    nc.vector.scalar_tensor_tensor(
+                        out=junk_v[:],
+                        in0=zt[:, KS - 1, :],
+                        scalar=1.0,
+                        in1=zt[:, KS - 1, :],
+                        op0=ALU.mult,
+                        op1=ALU.mult,
+                        accum_out=sqv[:, g // 2 : g // 2 + 1],
+                    )
+                if g == G - 1 and kt == KT - 2:
+                    for i in range(NG):
+                        nc.vector.scalar_tensor_tensor(
+                            out=junk_d[:],
+                            in0=grams[i][:],
+                            scalar=1.0,
+                            in1=ident[:],
+                            op0=ALU.mult,
+                            op1=ALU.mult,
+                            accum_out=ssq[:, KS + i : KS + i + 1],
+                        )
+
+        gw = big.tile([P, 2, C, 4], BF16, tag="big", name="gw", align_bytes=64)
+
+        def w_bank(n):
+            c, ct = divmod(n, C // P)
+            pw = psum.tile([P, 4, P], BF16, tag="ps", name="pw")
+            for t in range(4):
+                kt = 4 * c + t
+                nc.tensor.transpose(pw[:, t, :], wn[:, ct, tile_cols(kt)], ident[:])
+            nc.scalar.copy(
+                out=gw[:, c, ct * P : (ct + 1) * P, :], in_=pw[:].rearrange("p t n -> p n t")
+            )
+
+        for n in range(W_EARLY):
+            w_bank(n)
+
+        ssum = const.tile([P, KT], F32, name="ssum")
+        nc.vector.tensor_reduce(out=ssum[:], in_=s1[:], axis=AX.X, op=ALU.add)
+        sv = const.tile([P, 1], F32, name="sv")
+        nc.vector.tensor_reduce(out=sv[:], in_=sqv[:], axis=AX.X, op=ALU.add)
+        nc.vector.tensor_reduce(out=ssq[:, 0:KS], in_=sq[:], axis=AX.X, op=ALU.add)
+        nc.vector.tensor_tensor(
+            out=ssq[:, KS - 1 : KS], in0=ssq[:, KS - 1 : KS], in1=sv[:], op=ALU.add
+        )
+        m2 = const.tile([P, KT], F32, name="m2")
+        nc.vector.scalar_tensor_tensor(
+            out=m2[:], in0=ssum[:], scalar=1.0 / (B * B), in1=ssum[:], op0=ALU.mult, op1=ALU.mult
+        )
+        var = const.tile([P, KT], F32, name="var")
+        nc.vector.scalar_tensor_tensor(
+            out=var[:], in0=ssq[:], scalar=1.0 / B, in1=m2[:], op0=ALU.mult, op1=ALU.subtract
+        )
+        ve = const.tile([P, KT], F32, name="ve")
+        nc.vector.tensor_scalar(
+            out=ve[:], in0=var[:], scalar1=0.0, scalar2=BN_EPS, op0=ALU.max, op1=ALU.add
+        )
+        sd = const.tile([P, KT], F32, name="sd")
+        nc.scalar.activation(out=sd[:], in_=ve[:], func=ACT.Sqrt)
+        for n in range(W_EARLY, 2 * C // P):
+            w_bank(n)
+        mean = const.tile([P, KT], F32, name="mean")
+        nc.vector.tensor_scalar(out=mean[:], in0=ssum[:], scalar1=1.0 / B, scalar2=None, op0=ALU.mult)
+        rstd = const.tile([P, KT], F32, name="rstd")
+        nc.vector.reciprocal(out=rstd[:], in_=sd[:])
+        a = const.tile([P, KT], F32, name="a")
+        nc.vector.tensor_tensor(out=a[:], in0=gb[:, 0:KT], in1=rstd[:], op=ALU.mult)
+        ma = const.tile([P, KT], F32, name="ma")
+        nc.vector.tensor_tensor(out=ma[:], in0=mean[:], in1=a[:], op=ALU.mult)
+        bb = const.tile([P, KT], F32, name="bb")
+        nc.vector.tensor_tensor(out=bb[:], in0=gb[:, KT : 2 * KT], in1=ma[:], op=ALU.subtract)
+
+        ghs = {}
+        cds = {}
+        scs = {}
+        accs = {}
+        lts = {}
+        negs = {}
+        esums = {}
+        lnt = {}
+        lne = {}
+        lnq = {}
+        shifts = {}
+
+        def affine(g, kts):
+            for kt in kts:
+                nc.vector.tensor_scalar(
+                    out=zts[g][:, kt, :],
+                    in0=zts[g][:, kt, :],
+                    scalar1=a[:, kt : kt + 1],
+                    scalar2=bb[:, kt : kt + 1],
+                    op0=ALU.mult,
+                    op1=ALU.add,
+                )
+
+        def regroup(u):
+            g, h = divmod(u, 2)
+            gh = grp.tile([P, 2, UB, 4], BF16, tag="gr", name="gh", align_bytes=64)
+            ghs[u] = gh
+            if u == 0:
+                shares = ((0, 0, UB, True), (1, 0, UB, True))
+            else:
+                shares = ((0, 0, UB, False), (1, 0, UB - R_V_COLS, False), (1, UB - R_V_COLS, UB, True))
+            for c, b0, b1, on_vector in shares:
+                dst = gh[:, c, b0:b1, :].rearrange("p (n i) t -> p n t i", i=4)
+                src = zts[g][:, 4 * c : 4 * c + 4, h * UB + b0 : h * UB + b1].rearrange(
+                    "p t (n i) -> p n t i", i=4
+                )
+                if on_vector:
+                    nc.vector.tensor_scalar(out=dst, in0=src, scalar1=0.0, scalar2=None, op0=ALU.max)
+                else:
+                    nc.scalar.activation(out=dst, in_=src, func=ACT.Relu)
+
+        def quant(u):
+            cd = cod.tile([P, 2 * UB], U32, tag="cd", name="cd", align_bytes=64)
+            sc = cod.tile([P, 2 * UB], U8, tag="sc", name="sc", align_bytes=64)
+            cds[u] = cd
+            scs[u] = sc
+            nc.vector.quantize_mx(
+                out=cd[:].bitcast(FP8X4),
+                scales=sc[:],
+                in_=ghs[u][:].rearrange("p c b t -> p (c b t)"),
+            )
+
+        def mx(u):
+            for jj in range(JH):
+                acc = psum.tile([P, C], F32, tag="ps", name="acc")
+                accs[(u, jj)] = acc
+                for c in range(2):
+                    col = c * UB + jj * P
+                    nc.tensor.matmul_mx(
+                        out=acc[:],
+                        lhsT=cds[u][:, col : col + P].bitcast(FP8X4),
+                        lhsT_scale=scs[u][:, col : col + P],
+                        rhs=wcodes[:, c * C : (c + 1) * C].bitcast(FP8X4),
+                        rhs_scale=wscl[:, c * C : (c + 1) * C],
+                        start=(c == 0),
+                        stop=(c == 1),
+                    )
+
+        def add_bias(u, tiles):
+            g, h = divmod(u, 2)
+            if h == 0 and tiles[0] == 0:
+                lts[g] = big.tile([P, J, C], F32, tag="big", name="lt", align_bytes=64)
+                negs[g] = small.tile([P, J], F32, name="neg_m")
+                esums[g] = small.tile([P, J], F32, name="esum")
+            lt = lts[g]
+            for jj in tiles:
+                nc.vector.tensor_tensor(
+                    out=lt[:, h * JH + jj, :], in0=accs[(u, jj)][:], in1=bias_bc[:], op=ALU.add
+                )
+
+        def row_max(u, jj0, jj1):
+            g, h = divmod(u, 2)
+            nc.vector.tensor_reduce(
+                out=negs[g][:, h * JH + jj0 : h * JH + jj1],
+                in_=lts[g][:, h * JH + jj0 : h * JH + jj1, :],
+                axis=AX.X,
+                op=ALU.max,
+                negate=True,
+            )
+
+        def expsum(u):
+            g, h = divmod(u, 2)
+            for jj in range(JH):
+                j = h * JH + jj
+                nc.scalar.activation(
+                    out=junk_e[:],
+                    in_=lts[g][:, j, :],
+                    func=ACT.Exp,
+                    bias=negs[g][:, j : j + 1],
+                    scale=1.0,
+                    accum_out=esums[g][:, j : j + 1],
+                )
+
+        def ln_guess(g, j0, j1):
+            n = j1 - j0
+            r_pos = small.tile([P, J], F32, name="r_pos")
+            nc.gpsimd.tensor_tensor(
+                out=r_pos[:, 0:n], in0=esums[g][:, j0:j1], in1=pe_pos[:, 0:n], op=ALU.pow
+            )
+            r_neg = small.tile([P, J], F32, name="r_neg")
+            nc.gpsimd.tensor_tensor(
+                out=r_neg[:, 0:n], in0=esums[g][:, j0:j1], in1=pe_neg[:, 0:n], op=ALU.pow
+            )
+            t = small.tile([P, J], F32, name="t")
+            lnt[(g, j0)] = t
+            nc.gpsimd.tensor_tensor(
+                out=t[:, 0:n], in0=r_pos[:, 0:n], in1=r_neg[:, 0:n], op=ALU.subtract
+            )
+            q = small.tile([P, J], F32, name="q")
+            nc.gpsimd.tensor_scalar(
+                out=q[:, 0:n],
+                in0=t[:, 0:n],
+                scalar1=-0.5 * ROOT,
+                scalar2=1.0,
+                op0=ALU.mult,
+                op1=ALU.add,
+            )
+            q2 = small.tile([P, J], F32, name="q2")
+            lnq[(g, j0)] = q2
+            nc.gpsimd.tensor_tensor(
+                out=q2[:, 0:n], in0=q[:, 0:n], in1=negs[g][:, j0:j1], op=ALU.add
+            )
+
+        def ln_step(g, j0, j1):
+            n = j1 - j0
+            e = small.tile([P, J], F32, name="e")
+            nc.scalar.activation(
+                out=e[:, 0:n], in_=lnt[(g, j0)][:, 0:n], func=ACT.Exp, scale=-0.5 * ROOT
+            )
+            w = small.tile([P, J], F32, name="w")
+            nc.gpsimd.tensor_tensor(
+                out=w[:, 0:n], in0=esums[g][:, j0:j1], in1=e[:, 0:n], op=ALU.mult
+            )
+            neg_c = small.tile([P, J], F32, name="neg_c")
+            shifts[(g, j0)] = neg_c
+            nc.gpsimd.tensor_tensor(
+                out=neg_c[:, 0:n], in0=lnq[(g, j0)][:, 0:n], in1=w[:, 0:n], op=ALU.subtract
+            )
+
+        def ln_table(g, j0, j1):
+            y = small.tile([P, J], F32, name="y")
+            lne[(g, j0)] = y
+            nc.scalar.activation(out=y[:, 0 : j1 - j0], in_=esums[g][:, j0:j1], func=ACT.Ln)
+
+        def ln_table_shift(g, j0, j1):
+            n = j1 - j0
+            neg_c = small.tile([P, J], F32, name="neg_c")
+            shifts[(g, j0)] = neg_c
+            nc.vector.tensor_tensor(
+                out=neg_c[:, 0:n], in0=negs[g][:, j0:j1], in1=lne[(g, j0)][:, 0:n], op=ALU.subtract
+            )
+
+        def subtract_store(g, h, key, engines):
+            lt = lts[g]
+            for jj in range(JH):
+                j = h * JH + jj
+                shift = shifts[key][:, j - key[1] : j - key[1] + 1]
+                engine = engines[jj]
+                if engine == "V":
+                    nc.vector.tensor_scalar(
+                        out=lt[:, j, :], in0=lt[:, j, :], scalar1=shift, scalar2=None, op0=ALU.add
+                    )
+                elif engine == "G":
+                    nc.gpsimd.tensor_scalar(
+                        out=lt[:, j, :],
+                        in0=lt[:, j, :],
+                        scalar1=1.0,
+                        scalar2=shift,
+                        op0=ALU.mult,
+                        op1=ALU.add,
+                    )
+                else:
+                    nc.scalar.activation(
+                        out=lt[:, j, :], in_=lt[:, j, :], func=ACT.Identity, bias=shift, scale=1.0
+                    )
+            u = 2 * g + h
+            nc.sync.dma_start(
+                out=out[u * UB : (u + 1) * UB, :].rearrange("(p j) c -> p j c", j=JH),
+                in_=lt[:, h * JH : (h + 1) * JH, :],
+            )
+
+        affine(0, range(KT))
+        regroup(0)
+        regroup(1)
+        nc.vector.quantize_mx(
+            out=wcodes[:].bitcast(FP8X4),
+            scales=wscl[:],
+            in_=gw[:].rearrange("p c n t -> p (c n t)"),
+        )
+        quant(0)
+        mx(0)
+        affine(1, range(KT))
+        for v in range(U + 1):
+            if v + 1 < U:
+                quant(v + 1)
+                mx(v + 1)
+            if v < U - 1:
+                add_bias(v, range(JH))
+            if v == U - 1:
+                for jj in range(JH):
+                    add_bias(v, range(jj, jj + 1))
+                    if jj >= 1:
+                        row_max(v, jj - 1, jj)
+                row_max(v, JH - 1, JH)
+            if v >= 1:
+                expsum(v - 1)
+            gf, odd = divmod(v - 2, 2)
+            if v >= 2 and odd == 0 and gf < G - 1:
+                ln_guess(gf, 0, J)
+            if v >= 3 and odd == 1:
+                ln_step(gf, 0, J)
+            if v == U:
+                ln_table(G - 1, 0, J)
+            if v + 2 < U:
+                regroup(v + 2)
+            if v + 4 < U:
+                half = range(0, 4) if v % 2 == 0 else range(4, KT)
+                affine((v + 4) // 2, half)
+            if v < U - 1:
+                row_max(v, 0, JH)
+            if v >= 3 and odd == 1:
+                subtract_store(gf, 0, (gf, 0), "GGGG" if v < U - 2 else "SSSS")
+            if v >= 4 and odd == 0:
+                subtract_store(gf - 1, 1, (gf - 1, 0), "GGGG" if v < U - 2 else "VVVV")
+            if v == U:
+                ln_table_shift(G - 1, 0, J)
+                subtract_store(G - 1, 0, (G - 1, 0), "VVVV")
+                subtract_store(G - 1, 1, (G - 1, 0), "SSVV")

@@ -33,7 +33,12 @@ N_WARM = 12
 R_V_COLS = 128
 G_W = 1
 W_EARLY = 2
-GRAM_RUN = 4
+PAD = 16
+ROWB = PASS_K + PAD
+SLOT = KS * GB + J * ROWB
+GRAM_RUNS_FIRST = (0, 0, 8, 8, 8)
+GRAM_RUNS = (5, 5, 5, 5, 4)
+GRAM_RUNS_LAST = (6, 6, 6, 6, 0)
 
 FLOPS = 2 * B * K * C
 
@@ -47,7 +52,8 @@ def tile_binarymlp_pb_t_kernel(tc, z2, g2, beta2, W3, b3, out):
     nc = tc.nc
     with ExitStack() as ctx:
         const = ctx.enter_context(tc.tile_pool(name="const", bufs=1))
-        big = ctx.enter_context(tc.tile_pool(name="big", bufs=11))
+        big = ctx.enter_context(tc.tile_pool(name="big", bufs=8))
+        st = ctx.enter_context(tc.tile_pool(name="st", bufs=4))
         grp = ctx.enter_context(tc.tile_pool(name="grp", bufs=2))
         cod = ctx.enter_context(tc.tile_pool(name="cod", bufs=4))
         small = ctx.enter_context(tc.tile_pool(name="small", bufs=4))
@@ -91,10 +97,9 @@ def tile_binarymlp_pb_t_kernel(tc, z2, g2, beta2, W3, b3, out):
         pe_neg = const.tile([P, J], F32, name="pe_neg")
         nc.gpsimd.memset(pe_neg[:], -1.0 / ROOT)
 
-        s1 = const.tile([P, KT, G], F32, name="s1")
+        s1 = const.tile([P, KS, G], F32, name="s1")
+        ssum = const.tile([P, KT], F32, name="ssum")
         sq = const.tile([P, KS, G], F32, name="sq")
-        nc.vector.memset(sq[:], 0.0)
-        sqv = const.tile([P, G // 2], F32, name="sqv")
         junk_v = const.tile([P, GB], BF16, name="junk_v")
         ssq = const.tile([P, KT], F32, name="ssq")
         junk_s = const.tile([P, GB], BF16, name="junk_s")
@@ -104,7 +109,7 @@ def tile_binarymlp_pb_t_kernel(tc, z2, g2, beta2, W3, b3, out):
         bias_bc = const.tile([P, C], F32, name="bias_bc")
         grams = []
         for i in range(NG):
-            grams.append(psum.tile([P, P], F32, tag="ps", name="gram%d" % i))
+            grams.append(psum.tile([P, P + 1], F32, tag="ps", name="gram%d" % i))
 
         pv = psum.tile([P, 4, P], BF16, tag="ps", name="pv")
         for t in range(4):
@@ -116,40 +121,61 @@ def tile_binarymlp_pb_t_kernel(tc, z2, g2, beta2, W3, b3, out):
         nc.tensor.matmul(out=pb[:], lhsT=ones[:], rhs=brow[:], start=True, stop=True)
         nc.scalar.copy(out=bias_bc[:], in_=pb[:])
 
-        zts = []
+        ztas = []
+        znbs = []
         gram_jobs = [(i, j) for i in range(NG) for j in range(J)]
         for g in range(G):
-            zt = big.tile([P, KT, GB], BF16, tag="big", name="zt%d" % g, align_bytes=64)
-            zts.append(zt)
-            zn = big.tile([P, J, K], BF16, tag="big", name="zn", align_bytes=64)
-            pieces = 2 if g == 0 else 1
-            for piece in range(pieces):
-                cols = slice(piece * K // pieces, (piece + 1) * K // pieces)
+            gt = big.tile([P, SLOT], BF16, tag="big", name="gt%d" % g, align_bytes=64)
+            zta = gt[:, 0 : KS * GB].rearrange("p (t b) -> p t b", t=KS)
+            znb = gt[:, KS * GB : SLOT].rearrange("p (j x) -> p j x", x=ROWB)
+            ztas.append(zta)
+            znbs.append(znb)
+            nc.gpsimd.memset(znb[:, :, PASS_K:ROWB], 1.0)
+            zna = st.tile([P, J, PASS_K], BF16, tag="st", name="zna", align_bytes=64)
+            for c in range(2):
                 for h in range(2):
                     u = 2 * g + h
                     nc.sync.dma_start(
-                        out=zn[:, h * JH : (h + 1) * JH, cols],
-                        in_=z2[u * UB : (u + 1) * UB, cols].rearrange("(p j) k -> p j k", j=JH),
+                        out=(zna[:, h * JH : (h + 1) * JH, :] if c == 0 else znb[:, h * JH : (h + 1) * JH, 0:PASS_K]),
+                        in_=z2[u * UB : (u + 1) * UB, c * PASS_K : (c + 1) * PASS_K].rearrange(
+                            "(p j) k -> p j k", j=JH
+                        ),
                     )
             if g == G_W:
-                wn = big.tile([P, C // P, K], BF16, tag="big", name="wn", align_bytes=64)
+                wn = st.tile([P, C // P, K], BF16, tag="st", name="wn", align_bytes=64)
                 nc.sync.dma_start(out=wn[:], in_=W3.rearrange("(t p) k -> p t k", p=P))
-            for kt in range(KT):
-                ks = tile_cols(kt)
+            runs = GRAM_RUNS_FIRST if g == 0 else (GRAM_RUNS_LAST if g == G - 1 else GRAM_RUNS)
+            for kt in range(KS):
                 pt = psum.tile([P, GB], BF16, tag="ps", name="pt")
                 for j in range(J):
-                    nc.tensor.transpose(pt[:, j * P : (j + 1) * P], zn[:, j, ks], ident[:])
-                for i, j in gram_jobs[GRAM_RUN * kt : GRAM_RUN * (kt + 1)]:
-                    gs = tile_cols(KS + i)
+                    nc.tensor.transpose(
+                        pt[:, j * P : (j + 1) * P],
+                        zna[:, j, kt:PASS_K:4] if kt < 4 else znb[:, j, 0:PASS_K:4],
+                        ident[:],
+                    )
+                for i, j in gram_jobs[sum(runs[0:kt]) : sum(runs[0 : kt + 1])]:
+                    t = KS + i - 4
                     nc.tensor.matmul(
                         out=grams[i][:],
-                        lhsT=zn[:, j, gs],
-                        rhs=zn[:, j, gs],
+                        lhsT=znb[:, j, t:PASS_K:4],
+                        rhs=znb[:, j, t : PASS_K + 4 : 4],
                         start=(g == 0 and j == 0),
                         stop=(g == G - 1 and j == J - 1),
                     )
+                if g == G - 1 and kt == KS - 1:
+                    for i in range(NG):
+                        nc.vector.scalar_tensor_tensor(
+                            out=junk_d[:],
+                            in0=grams[i][:, 0:P],
+                            scalar=1.0,
+                            in1=ident[:],
+                            op0=ALU.mult,
+                            op1=ALU.mult,
+                            accum_out=ssq[:, KS + i : KS + i + 1],
+                        )
+                        nc.vector.tensor_copy(out=ssum[:, KS + i : KS + i + 1], in_=grams[i][:, P : P + 1])
                 nc.vector.tensor_scalar(
-                    out=zt[:, kt, :],
+                    out=zta[:, kt, :],
                     in0=pt[:],
                     scalar1=1.0,
                     scalar2=None,
@@ -157,36 +183,35 @@ def tile_binarymlp_pb_t_kernel(tc, z2, g2, beta2, W3, b3, out):
                     op1=ALU.add,
                     accum_out=s1[:, kt, g : g + 1],
                 )
-                if kt < KS - 1 or (kt == KS - 1 and g % 2 == 0):
+                if kt < KS - 1:
                     nc.scalar.activation(
                         out=junk_s[:],
-                        in_=zt[:, kt, :],
+                        in_=zta[:, kt, :],
                         func=ACT.Square,
                         accum_out=sq[:, kt, g : g + 1],
                     )
-                if kt == KS and g % 2 == 1:
+                else:
                     nc.vector.scalar_tensor_tensor(
                         out=junk_v[:],
-                        in0=zt[:, KS - 1, :],
+                        in0=zta[:, kt, :],
                         scalar=1.0,
-                        in1=zt[:, KS - 1, :],
+                        in1=zta[:, kt, :],
                         op0=ALU.mult,
                         op1=ALU.mult,
-                        accum_out=sqv[:, g // 2 : g // 2 + 1],
+                        accum_out=sq[:, kt, g : g + 1],
                     )
-                if g == G - 1 and kt == KT - 2:
-                    for i in range(NG):
-                        nc.vector.scalar_tensor_tensor(
-                            out=junk_d[:],
-                            in0=grams[i][:],
-                            scalar=1.0,
-                            in1=ident[:],
-                            op0=ALU.mult,
-                            op1=ALU.mult,
-                            accum_out=ssq[:, KS + i : KS + i + 1],
-                        )
+        dts = {}
 
-        gw = big.tile([P, 2, C, 4], BF16, tag="big", name="gw", align_bytes=64)
+        def late_transposes(g):
+            for i in range(NG):
+                dt = psum.tile([P, GB], BF16, tag="ps", name="dt")
+                dts[(g, i)] = dt
+                for j in range(J):
+                    nc.tensor.transpose(dt[:, j * P : (j + 1) * P], znbs[g][:, j, KS + i - 4 : PASS_K : 4], ident[:])
+
+        late_transposes(0)
+
+        gw = st.tile([P, 2, C, 4], BF16, tag="st", name="gw", align_bytes=64)
 
         def w_bank(n):
             c, ct = divmod(n, C // P)
@@ -201,14 +226,8 @@ def tile_binarymlp_pb_t_kernel(tc, z2, g2, beta2, W3, b3, out):
         for n in range(W_EARLY):
             w_bank(n)
 
-        ssum = const.tile([P, KT], F32, name="ssum")
-        nc.vector.tensor_reduce(out=ssum[:], in_=s1[:], axis=AX.X, op=ALU.add)
-        sv = const.tile([P, 1], F32, name="sv")
-        nc.vector.tensor_reduce(out=sv[:], in_=sqv[:], axis=AX.X, op=ALU.add)
+        nc.vector.tensor_reduce(out=ssum[:, 0:KS], in_=s1[:], axis=AX.X, op=ALU.add)
         nc.vector.tensor_reduce(out=ssq[:, 0:KS], in_=sq[:], axis=AX.X, op=ALU.add)
-        nc.vector.tensor_tensor(
-            out=ssq[:, KS - 1 : KS], in0=ssq[:, KS - 1 : KS], in1=sv[:], op=ALU.add
-        )
         m2 = const.tile([P, KT], F32, name="m2")
         nc.vector.scalar_tensor_tensor(
             out=m2[:], in0=ssum[:], scalar=1.0 / (B * B), in1=ssum[:], op0=ALU.mult, op1=ALU.mult
@@ -225,6 +244,8 @@ def tile_binarymlp_pb_t_kernel(tc, z2, g2, beta2, W3, b3, out):
         nc.scalar.activation(out=sd[:], in_=ve[:], func=ACT.Sqrt)
         for n in range(W_EARLY, 2 * C // P):
             w_bank(n)
+
+        late_transposes(1)
         mean = const.tile([P, KT], F32, name="mean")
         nc.vector.tensor_scalar(out=mean[:], in0=ssum[:], scalar1=1.0 / B, scalar2=None, op0=ALU.mult)
         rstd = const.tile([P, KT], F32, name="rstd")
@@ -248,11 +269,16 @@ def tile_binarymlp_pb_t_kernel(tc, z2, g2, beta2, W3, b3, out):
         lnq = {}
         shifts = {}
 
-        def affine(g, kts):
-            for kt in kts:
+        ztbs = {}
+
+        def affine(g, c):
+            if c == 1:
+                ztbs[g] = st.tile([P, 4, GB], BF16, tag="st", name="ztb", align_bytes=64)
+            for t in range(4):
+                kt = 4 * c + t
                 nc.vector.tensor_scalar(
-                    out=zts[g][:, kt, :],
-                    in0=zts[g][:, kt, :],
+                    out=ztas[g][:, kt, :] if c == 0 else ztbs[g][:, t, :],
+                    in0=ztas[g][:, kt, :] if kt < KS else dts[(g, kt - KS)][:],
                     scalar1=a[:, kt : kt + 1],
                     scalar2=bb[:, kt : kt + 1],
                     op0=ALU.mult,
@@ -269,9 +295,8 @@ def tile_binarymlp_pb_t_kernel(tc, z2, g2, beta2, W3, b3, out):
                 shares = ((0, 0, UB, False), (1, 0, UB - R_V_COLS, False), (1, UB - R_V_COLS, UB, True))
             for c, b0, b1, on_vector in shares:
                 dst = gh[:, c, b0:b1, :].rearrange("p (n i) t -> p n t i", i=4)
-                src = zts[g][:, 4 * c : 4 * c + 4, h * UB + b0 : h * UB + b1].rearrange(
-                    "p t (n i) -> p n t i", i=4
-                )
+                four = ztas[g][:, 0:4, :] if c == 0 else ztbs[g][:]
+                src = four[:, :, h * UB + b0 : h * UB + b1].rearrange("p t (n i) -> p n t i", i=4)
                 if on_vector:
                     nc.vector.tensor_scalar(out=dst, in0=src, scalar1=0.0, scalar2=None, op0=ALU.max)
                 else:
@@ -288,8 +313,8 @@ def tile_binarymlp_pb_t_kernel(tc, z2, g2, beta2, W3, b3, out):
                 in_=ghs[u][:].rearrange("p c b t -> p (c b t)"),
             )
 
-        def mx(u):
-            for jj in range(JH):
+        def mx(u, tiles):
+            for jj in tiles:
                 acc = psum.tile([P, C], F32, tag="ps", name="acc")
                 accs[(u, jj)] = acc
                 for c in range(2):
@@ -427,7 +452,8 @@ def tile_binarymlp_pb_t_kernel(tc, z2, g2, beta2, W3, b3, out):
                 in_=lt[:, h * JH : (h + 1) * JH, :],
             )
 
-        affine(0, range(KT))
+        affine(0, 0)
+        affine(0, 1)
         regroup(0)
         regroup(1)
         nc.vector.quantize_mx(
@@ -436,14 +462,18 @@ def tile_binarymlp_pb_t_kernel(tc, z2, g2, beta2, W3, b3, out):
             in_=gw[:].rearrange("p c n t -> p (c n t)"),
         )
         quant(0)
-        mx(0)
-        affine(1, range(KT))
+        mx(0, range(JH))
+        affine(1, 0)
+        affine(1, 1)
         for v in range(U + 1):
             if v + 1 < U:
                 quant(v + 1)
-                mx(v + 1)
             if v < U - 1:
-                add_bias(v, range(JH))
+                for jj in range(JH):
+                    add_bias(v, range(jj, jj + 1))
+                    mx(v + 1, range(jj, jj + 1))
+            if v % 2 == 0 and v + 4 < U:
+                late_transposes((v + 4) // 2)
             if v == U - 1:
                 for jj in range(JH):
                     add_bias(v, range(jj, jj + 1))
@@ -462,8 +492,7 @@ def tile_binarymlp_pb_t_kernel(tc, z2, g2, beta2, W3, b3, out):
             if v + 2 < U:
                 regroup(v + 2)
             if v + 4 < U:
-                half = range(0, 4) if v % 2 == 0 else range(4, KT)
-                affine((v + 4) // 2, half)
+                affine((v + 4) // 2, v % 2)
             if v < U - 1:
                 row_max(v, 0, JH)
             if v >= 3 and odd == 1:

@@ -25,27 +25,18 @@ U = 16
 UB = B // U
 JH = UB // P
 J = GB // P
-NG = 3
-KS = KT - NG
 BN_EPS = 1e-5
 ROOT = 1024.0
 N_WARM = 12
-R_V_COLS = 128
 G_W = 1
-W_EARLY = 2
-PAD = 16
-ROWB = PASS_K + PAD
-SLOT = KS * GB + J * ROWB
-GRAM_RUNS_FIRST = (0, 0, 8, 8, 8)
-GRAM_RUNS = (5, 5, 5, 5, 4)
-GRAM_RUNS_LAST = (6, 6, 6, 6, 0)
+G_WT = 3
+CHUNK = 256
+NCH = B // CHUNK
+NV = NCH + NCH // 2
+INV = 1.0 / CHUNK
+NG = 3
 
 FLOPS = 2 * B * K * C
-
-
-def tile_cols(kt):
-    c, t = divmod(kt, 4)
-    return slice(c * PASS_K + t, (c + 1) * PASS_K, 4)
 
 
 def tile_binarymlp_pb_t_kernel(tc, z2, g2, beta2, W3, b3, out):
@@ -54,10 +45,12 @@ def tile_binarymlp_pb_t_kernel(tc, z2, g2, beta2, W3, b3, out):
         const = ctx.enter_context(tc.tile_pool(name="const", bufs=1))
         big = ctx.enter_context(tc.tile_pool(name="big", bufs=8))
         st = ctx.enter_context(tc.tile_pool(name="st", bufs=4))
-        grp = ctx.enter_context(tc.tile_pool(name="grp", bufs=2))
-        cod = ctx.enter_context(tc.tile_pool(name="cod", bufs=4))
+        zsp = ctx.enter_context(tc.tile_pool(name="zsp", bufs=3))
+        grp = ctx.enter_context(tc.tile_pool(name="grp", bufs=3))
+        cod = ctx.enter_context(tc.tile_pool(name="cod", bufs=3))
         small = ctx.enter_context(tc.tile_pool(name="small", bufs=4))
-        psum = ctx.enter_context(tc.psum_pool(name="psum", bufs=8))
+        psa = ctx.enter_context(tc.psum_pool(name="psa", bufs=4))
+        pst = ctx.enter_context(tc.psum_pool(name="pst", bufs=4))
         ctx.enter_context(tc.manual_schedule())
 
         brow = const.tile([P, C], BF16, name="brow")
@@ -76,7 +69,7 @@ def tile_binarymlp_pb_t_kernel(tc, z2, g2, beta2, W3, b3, out):
         warm = const.tile([P, 1], F32, name="warm")
         nc.scalar.activation(out=warm[:], in_=one[:], func=ACT.Sqrt)
 
-        pwarm = psum.tile([P, C], F32, tag="ps", name="pwarm")
+        pwarm = psa.tile([P, C], F32, tag="acc", name="pwarm")
         for i in range(N_WARM):
             nc.tensor.matmul_mx(
                 out=pwarm[:],
@@ -90,151 +83,238 @@ def tile_binarymlp_pb_t_kernel(tc, z2, g2, beta2, W3, b3, out):
 
         ident = const.tile([P, P], BF16, name="ident")
         make_identity(nc, ident[:])
+        identf = const.tile([P, P], F32, name="identf")
+        make_identity(nc, identf[:])
         ones = const.tile([P, P], BF16, name="ones")
         nc.vector.memset(ones[:], 1.0)
+        inv_col = const.tile([P, 1], BF16, name="inv_col")
+        nc.vector.memset(inv_col[:], INV)
         pe_pos = const.tile([P, J], F32, name="pe_pos")
         nc.gpsimd.memset(pe_pos[:], 1.0 / ROOT)
-        pe_neg = const.tile([P, J], F32, name="pe_neg")
-        nc.gpsimd.memset(pe_neg[:], -1.0 / ROOT)
 
-        s1 = const.tile([P, KS, G], F32, name="s1")
-        ssum = const.tile([P, KT], F32, name="ssum")
-        sq = const.tile([P, KS, G], F32, name="sq")
-        junk_v = const.tile([P, GB], BF16, name="junk_v")
-        ssq = const.tile([P, KT], F32, name="ssq")
+        bs = const.tile([P, (NV + 1) * 6], F32, name="bs")
+        msq = const.tile([P, 2 * NV], F32, name="msq")
+        qsum = const.tile([P, 2, NV + G], F32, name="qsum")
+        sq = const.tile([P, U], F32, name="sq")
+        ab = const.tile([P, 4 * P], F32, name="ab", align_bytes=64)
+        nc.gpsimd.memset(ab[:], 0.0)
+        rows = const.tile([P, PASS_K], F32, name="rows", align_bytes=64)
+        nc.gpsimd.memset(rows[:], 0.0)
+        stat = const.tile([P, 2 * KT], F32, name="stat")
         junk_s = const.tile([P, GB], BF16, name="junk_s")
         junk_e = const.tile([P, C], BF16, name="junk_e")
         junk_d = const.tile([P, P], F32, name="junk_d")
         gb = const.tile([P, 2 * KT], F32, name="gb")
         bias_bc = const.tile([P, C], F32, name="bias_bc")
-        grams = []
-        for i in range(NG):
-            grams.append(psum.tile([P, P + 1], F32, tag="ps", name="gram%d" % i))
 
-        pv = psum.tile([P, 4, P], BF16, tag="ps", name="pv")
+        pv = pst.tile([P, 4, P], BF16, tag="tr", name="pv")
         for t in range(4):
             nc.tensor.transpose(pv[:, t, :], vecs[:, t:PASS_K:4], ident[:])
         nc.vector.tensor_copy(
             out=gb[:].rearrange("p (r t) -> p r t", t=4), in_=pv[:, :, 0:4].rearrange("p t r -> p r t")
         )
-        pb = psum.tile([P, C], F32, tag="ps", name="pb")
+        pb = pst.tile([P, C], F32, tag="tr", name="pb")
         nc.tensor.matmul(out=pb[:], lhsT=ones[:], rhs=brow[:], start=True, stop=True)
         nc.scalar.copy(out=bias_bc[:], in_=pb[:])
 
-        ztas = []
-        znbs = []
-        gram_jobs = [(i, j) for i in range(NG) for j in range(J)]
-        for g in range(G):
-            gt = big.tile([P, SLOT], BF16, tag="big", name="gt%d" % g, align_bytes=64)
-            zta = gt[:, 0 : KS * GB].rearrange("p (t b) -> p t b", t=KS)
-            znb = gt[:, KS * GB : SLOT].rearrange("p (j x) -> p j x", x=ROWB)
-            ztas.append(zta)
-            znbs.append(znb)
-            nc.gpsimd.memset(znb[:, :, PASS_K:ROWB], 1.0)
-            zna = st.tile([P, J, PASS_K], BF16, tag="st", name="zna", align_bytes=64)
-            for c in range(2):
-                for h in range(2):
-                    u = 2 * g + h
-                    nc.sync.dma_start(
-                        out=(zna[:, h * JH : (h + 1) * JH, :] if c == 0 else znb[:, h * JH : (h + 1) * JH, 0:PASS_K]),
-                        in_=z2[u * UB : (u + 1) * UB, c * PASS_K : (c + 1) * PASS_K].rearrange(
-                            "(p j) k -> p j k", j=JH
-                        ),
-                    )
-            if g == G_W:
-                wn = st.tile([P, C // P, K], BF16, tag="st", name="wn", align_bytes=64)
-                nc.sync.dma_start(out=wn[:], in_=W3.rearrange("(t p) k -> p t k", p=P))
-            runs = GRAM_RUNS_FIRST if g == 0 else (GRAM_RUNS_LAST if g == G - 1 else GRAM_RUNS)
-            for kt in range(KS):
-                pt = psum.tile([P, GB], BF16, tag="ps", name="pt")
-                for j in range(J):
-                    nc.tensor.transpose(
-                        pt[:, j * P : (j + 1) * P],
-                        zna[:, j, kt:PASS_K:4] if kt < 4 else znb[:, j, 0:PASS_K:4],
-                        ident[:],
-                    )
-                for i, j in gram_jobs[sum(runs[0:kt]) : sum(runs[0 : kt + 1])]:
-                    t = KS + i - 4
-                    nc.tensor.matmul(
-                        out=grams[i][:],
-                        lhsT=znb[:, j, t:PASS_K:4],
-                        rhs=znb[:, j, t : PASS_K + 4 : 4],
-                        start=(g == 0 and j == 0),
-                        stop=(g == G - 1 and j == J - 1),
-                    )
-                if g == G - 1 and kt == KS - 1:
-                    for i in range(NG):
-                        nc.vector.scalar_tensor_tensor(
-                            out=junk_d[:],
-                            in0=grams[i][:, 0:P],
-                            scalar=1.0,
-                            in1=ident[:],
-                            op0=ALU.mult,
-                            op1=ALU.mult,
-                            accum_out=ssq[:, KS + i : KS + i + 1],
-                        )
-                        nc.vector.tensor_copy(out=ssum[:, KS + i : KS + i + 1], in_=grams[i][:, P : P + 1])
-                nc.vector.tensor_scalar(
-                    out=zta[:, kt, :],
-                    in0=pt[:],
-                    scalar1=1.0,
-                    scalar2=None,
-                    op0=ALU.mult,
-                    op1=ALU.add,
-                    accum_out=s1[:, kt, g : g + 1],
-                )
-                if kt < KS - 1:
-                    nc.scalar.activation(
-                        out=junk_s[:],
-                        in_=zta[:, kt, :],
-                        func=ACT.Square,
-                        accum_out=sq[:, kt, g : g + 1],
-                    )
-                else:
-                    nc.vector.scalar_tensor_tensor(
-                        out=junk_v[:],
-                        in0=zta[:, kt, :],
-                        scalar=1.0,
-                        in1=zta[:, kt, :],
-                        op0=ALU.mult,
-                        op1=ALU.mult,
-                        accum_out=sq[:, kt, g : g + 1],
-                    )
-        dts = {}
-
-        def late_transposes(g):
-            for i in range(NG):
-                dt = psum.tile([P, GB], BF16, tag="ps", name="dt")
-                dts[(g, i)] = dt
-                for j in range(J):
-                    nc.tensor.transpose(dt[:, j * P : (j + 1) * P], znbs[g][:, j, KS + i - 4 : PASS_K : 4], ident[:])
-
-        late_transposes(0)
+        grams = []
+        for i in range(NG):
+            grams.append(psa.tile([P, P], F32, tag="acc", name="gram%d" % i))
+        psums = psa.tile([P, 6 * G], F32, tag="acc", name="psums")
+        plain = [(0, 0), (0, 1), (1, 0), (1, 1)]
+        cols = [c * PASS_K + 256 + h * P for c, h in plain]
+        n_v = [0, NCH]
 
         gw = st.tile([P, 2, C, 4], BF16, tag="st", name="gw", align_bytes=64)
 
         def w_bank(n):
-            c, ct = divmod(n, C // P)
-            pw = psum.tile([P, 4, P], BF16, tag="ps", name="pw")
-            for t in range(4):
-                kt = 4 * c + t
-                nc.tensor.transpose(pw[:, t, :], wn[:, ct, tile_cols(kt)], ident[:])
-            nc.scalar.copy(
-                out=gw[:, c, ct * P : (ct + 1) * P, :], in_=pw[:].rearrange("p t n -> p n t")
+            c, ct = divmod(2 * n, C // P)
+            ww = wn[:].bitcast(F32)
+            pw = pst.tile([P, 2, 2, P], F32, tag="tr", name="pw")
+            for i in range(2):
+                for u in range(2):
+                    nc.tensor.transpose(
+                        pw[:, i, u, :], ww[:, ct + i, 256 * c + u : 256 * (c + 1) : 2], identf[:]
+                    )
+            for i in range(2):
+                nc.scalar.copy(
+                    out=gw[:, c, (ct + i) * P : (ct + i + 1) * P, :].bitcast(F32),
+                    in_=pw[:, i, :, :].rearrange("p u n -> p n u"),
+                )
+
+        zns = []
+        for g in range(G):
+            zn = big.tile([P, J, K], BF16, tag="big", name="zn%d" % g, align_bytes=64)
+            zns.append(zn)
+            for h in range(2):
+                u = 2 * g + h
+                nc.sync.dma_start(
+                    out=zn[:, h * JH : (h + 1) * JH, :],
+                    in_=z2[u * UB : (u + 1) * UB, :].rearrange("(p j) k -> p j k", j=JH),
+                )
+            if g == G_W:
+                wn = st.tile([P, C // P, K], BF16, tag="st", name="wn", align_bytes=64)
+                nc.sync.dma_start(out=wn[:], in_=W3.rearrange("(t p) k -> p t k", p=P))
+            zw = zn[:].bitcast(F32)
+            for h in range(2):
+                u = 2 * g + h
+                if h == 0:
+                    pt = pst.tile([P, GB], BF16, tag="tr", name="pt")
+                for c in range(2):
+                    pw2 = pst.tile([P, JH * P], F32, tag="tr", name="pw2")
+                    for j in range(JH):
+                        nc.tensor.transpose(
+                            pw2[:, j * P : (j + 1) * P], zw[:, h * JH + j, 256 * c : 256 * c + P], identf[:]
+                        )
+                    for i in range(NG):
+                        for j in range(2 * c, 2 * c + 2):
+                            jj = h * JH + j
+                            nc.tensor.matmul(
+                                out=grams[i][:],
+                                lhsT=zn[:, jj, cols[i] : cols[i] + P],
+                                rhs=zn[:, jj, cols[i] : cols[i] + P],
+                                start=(g == 0 and jj == 0),
+                                stop=(g == G - 1 and jj == J - 1),
+                            )
+                    pb2 = pw2[:].bitcast(BF16)
+                    if c == 1 and h == 0:
+                        for e in range(2):
+                            nc.scalar.activation(
+                                out=junk_s[:, 0:UB],
+                                in_=pb2[:, e : 2 * UB : 2],
+                                func=ACT.Square,
+                                accum_out=qsum[:, e, NV + g : NV + g + 1],
+                            )
+                    else:
+                        for q in range(2):
+                            n = n_v[c] * 6
+                            n_v[c] += 1
+                            nc.vector.bn_stats(out=bs[:, n : n + 6], in_=pb2[:, q * 512 : (q + 1) * 512])
+                for j in range(h * JH, (h + 1) * JH):
+                    nc.tensor.transpose(pt[:, j * P : (j + 1) * P], zn[:, j, cols[3] : cols[3] + P], ident[:])
+                nc.scalar.activation(
+                    out=junk_s[:, 0:UB],
+                    in_=pt[:, h * UB : (h + 1) * UB],
+                    func=ACT.Square,
+                    accum_out=sq[:, u : u + 1],
+                )
+                if h == 0:
+                    for e in range(2):
+                        for j in range(JH):
+                            nc.tensor.matmul(
+                                out=psums[:, (4 + e) * G + g : (4 + e) * G + g + 1],
+                                lhsT=zn[:, j, PASS_K + e : PASS_K + 256 : 2],
+                                rhs=inv_col[:],
+                                start=(j == 0),
+                                stop=(j == JH - 1),
+                            )
+            for i in range(4):
+                for j in range(J):
+                    nc.tensor.matmul(
+                        out=psums[:, i * G + g : i * G + g + 1],
+                        lhsT=zn[:, j, cols[i] : cols[i] + P],
+                        rhs=inv_col[:],
+                        start=(j == 0),
+                        stop=(j == J - 1),
+                    )
+            if g >= G_WT and g < G_WT + 4:
+                w_bank(g - G_WT)
+            if g == G_WT + 3:
+                nc.vector.quantize_mx(
+                    out=wcodes[:].bitcast(FP8X4),
+                    scales=wscl[:],
+                    in_=gw[:].rearrange("p c n t -> p (c n t)"),
+                )
+
+        dts = {}
+        wts = {}
+
+        def late_tile(g, t):
+            dt = pst.tile([P, GB], BF16, tag="tr", name="dt")
+            dts[(g, t)] = dt
+            for j in range(J):
+                nc.tensor.transpose(dt[:, j * P : (j + 1) * P], zns[g][:, j, t:PASS_K:4], ident[:])
+
+        def late_words(v, u):
+            g, h = divmod(v, 2)
+            wt = pst.tile([P, UB], F32, tag="tr", name="wt")
+            wts[(v, u)] = wt
+            zw = zns[g][:].bitcast(F32)
+            for j in range(JH):
+                nc.tensor.transpose(
+                    wt[:, j * P : (j + 1) * P], zw[:, h * JH + j, 256 + u : 512 : 2], identf[:]
+                )
+
+        late_tile(0, 0)
+        late_tile(0, 1)
+        late_words(0, 0)
+        late_words(0, 1)
+
+        abv = ab[:].rearrange("p (u h x) -> p u h x", u=2, h=2)
+        bsv = bs[:].rearrange("p (n e f) -> p e n f", e=2, f=3)
+        mean_v = bsv[:, :, 0:NV, 1]
+        nc.vector.tensor_reduce(
+            out=bsv[:, :, NV, 1],
+            in_=psums[:, 4 * G : 6 * G].rearrange("p (e g) -> p e g", e=2),
+            axis=AX.X,
+            op=ALU.add,
+        )
+        nc.vector.tensor_tensor(
+            out=msq[:].rearrange("p (e n) -> p e n", e=2), in0=mean_v, in1=mean_v, op=ALU.mult
+        )
+        for c, n0, n1 in ((0, 0, NCH), (1, NCH, NV + 1)):
+            nc.vector.tensor_reduce(out=abv[:, 0, :, c], in_=bsv[:, :, n0:n1, 1], axis=AX.X, op=ALU.add)
+        nc.vector.scalar_tensor_tensor(
+            out=qsum[:, :, 0:NV],
+            in0=msq[:].rearrange("p (e n) -> p e n", e=2),
+            scalar=float(CHUNK),
+            in1=bsv[:, :, 0:NV, 2],
+            op0=ALU.mult,
+            op1=ALU.add,
+        )
+        for i in range(NG):
+            c, h = plain[i]
+            nc.vector.scalar_tensor_tensor(
+                out=junk_d[:],
+                in0=grams[i][:],
+                scalar=1.0,
+                in1=ident[:],
+                op0=ALU.mult,
+                op1=ALU.mult,
+                accum_out=abv[:, 1, h, 2 + c : 3 + c],
             )
-
-        for n in range(W_EARLY):
-            w_bank(n)
-
-        nc.vector.tensor_reduce(out=ssum[:, 0:KS], in_=s1[:], axis=AX.X, op=ALU.add)
-        nc.vector.tensor_reduce(out=ssq[:, 0:KS], in_=sq[:], axis=AX.X, op=ALU.add)
+        for c, n0, n1 in ((0, 0, NCH), (1, NCH, NV + G)):
+            nc.vector.tensor_reduce(out=abv[:, 0, :, 2 + c], in_=qsum[:, :, n0:n1], axis=AX.X, op=ALU.add)
+        nc.vector.tensor_reduce(
+            out=abv[:, 1, :, 0:2],
+            in_=psums[:, 0 : 4 * G].rearrange("p (c h g) -> p h c g", c=2, h=2),
+            axis=AX.X,
+            op=ALU.add,
+        )
+        nc.vector.tensor_reduce(out=abv[:, 1, 1, 3:4], in_=sq[:], axis=AX.X, op=ALU.add)
+        pt1 = psa.tile([P, 4 * P], F32, tag="acc", name="pt1")
+        for q in range(4):
+            nc.tensor.transpose(pt1[:, q * P : (q + 1) * P], ab[:, q * P : (q + 1) * P], identf[:])
+        nc.vector.tensor_copy(
+            out=rows[0:4, 0:256].rearrange("r (q e) -> r q e", e=2),
+            in_=pt1[0:4, 0:256].rearrange("r (e q) -> r q e", e=2),
+        )
+        nc.vector.tensor_copy(out=rows[0:4, 256:512], in_=pt1[0:4, 256:512])
+        pt2 = psa.tile([P, 4, P], F32, tag="acc", name="pt2")
+        for t in range(4):
+            nc.tensor.transpose(pt2[:, t, :], rows[:, t:PASS_K:4], identf[:])
+        nc.vector.tensor_copy(
+            out=stat[:].rearrange("p (r t) -> p r t", t=4), in_=pt2[:, :, 0:4].rearrange("p t r -> p r t")
+        )
+        ssum = stat[:, 0:KT]
+        ssq = stat[:, KT : 2 * KT]
         m2 = const.tile([P, KT], F32, name="m2")
         nc.vector.scalar_tensor_tensor(
-            out=m2[:], in0=ssum[:], scalar=1.0 / (B * B), in1=ssum[:], op0=ALU.mult, op1=ALU.mult
+            out=m2[:], in0=ssum, scalar=float(CHUNK * CHUNK) / (B * B), in1=ssum, op0=ALU.mult, op1=ALU.mult
         )
         var = const.tile([P, KT], F32, name="var")
         nc.vector.scalar_tensor_tensor(
-            out=var[:], in0=ssq[:], scalar=1.0 / B, in1=m2[:], op0=ALU.mult, op1=ALU.subtract
+            out=var[:], in0=ssq, scalar=1.0 / B, in1=m2[:], op0=ALU.mult, op1=ALU.subtract
         )
         ve = const.tile([P, KT], F32, name="ve")
         nc.vector.tensor_scalar(
@@ -242,12 +322,11 @@ def tile_binarymlp_pb_t_kernel(tc, z2, g2, beta2, W3, b3, out):
         )
         sd = const.tile([P, KT], F32, name="sd")
         nc.scalar.activation(out=sd[:], in_=ve[:], func=ACT.Sqrt)
-        for n in range(W_EARLY, 2 * C // P):
-            w_bank(n)
-
-        late_transposes(1)
+        nc.scalar.activation(out=warm[:], in_=one[:], func=ACT.Exp)
         mean = const.tile([P, KT], F32, name="mean")
-        nc.vector.tensor_scalar(out=mean[:], in0=ssum[:], scalar1=1.0 / B, scalar2=None, op0=ALU.mult)
+        nc.vector.tensor_scalar(
+            out=mean[:], in0=ssum, scalar1=float(CHUNK) / B, scalar2=None, op0=ALU.mult
+        )
         rstd = const.tile([P, KT], F32, name="rstd")
         nc.vector.reciprocal(out=rstd[:], in_=sd[:])
         a = const.tile([P, KT], F32, name="a")
@@ -264,85 +343,99 @@ def tile_binarymlp_pb_t_kernel(tc, z2, g2, beta2, W3, b3, out):
         lts = {}
         negs = {}
         esums = {}
+        rpos = {}
+        rneg = {}
         lnt = {}
         lne = {}
         lnq = {}
         shifts = {}
+        ztas = {}
+        zss = {}
 
-        ztbs = {}
+        def affine_v(g, t):
+            if t == 0:
+                ztas[g] = st.tile([P, 4, GB], BF16, tag="st", name="zta", align_bytes=64)
+            nc.vector.tensor_scalar(
+                out=ztas[g][:, t, :],
+                in0=dts[(g, t)][:],
+                scalar1=a[:, t : t + 1],
+                scalar2=bb[:, t : t + 1],
+                op0=ALU.mult,
+                op1=ALU.add,
+            )
 
-        def affine(g, c):
-            if c == 1:
-                ztbs[g] = st.tile([P, 4, GB], BF16, tag="st", name="ztb", align_bytes=64)
-            for t in range(4):
-                kt = 4 * c + t
-                nc.vector.tensor_scalar(
-                    out=ztas[g][:, kt, :] if c == 0 else ztbs[g][:, t, :],
-                    in0=ztas[g][:, kt, :] if kt < KS else dts[(g, kt - KS)][:],
-                    scalar1=a[:, kt : kt + 1],
-                    scalar2=bb[:, kt : kt + 1],
-                    op0=ALU.mult,
-                    op1=ALU.add,
-                )
+        def affine_s(v):
+            zss[v] = zsp.tile([P, 4, UB], BF16, tag="zs", name="zs", align_bytes=64)
+            for u in range(2):
+                pairs = wts[(v, u)][:].bitcast(BF16)
+                for e in range(2):
+                    kt = 4 + 2 * u + e
+                    nc.scalar.activation(
+                        out=zss[v][:, 2 * u + e, :],
+                        in_=pairs[:, e : 2 * UB : 2],
+                        func=ACT.Relu,
+                        bias=bb[:, kt : kt + 1],
+                        scale=a[:, kt : kt + 1],
+                    )
 
-        def regroup(u):
-            g, h = divmod(u, 2)
-            gh = grp.tile([P, 2, UB, 4], BF16, tag="gr", name="gh", align_bytes=64)
-            ghs[u] = gh
-            if u == 0:
-                shares = ((0, 0, UB, True), (1, 0, UB, True))
+        def regroup(v, c, b0, b1, engine):
+            g, h = divmod(v, 2)
+            if v not in ghs:
+                ghs[v] = grp.tile([P, 2, UB, 4], BF16, tag="gr", name="gh", align_bytes=64)
+            four = ztas[g][:, :, h * UB : (h + 1) * UB] if c == 0 else zss[v][:]
+            if engine == "G":
+                dst = ghs[v][:, c, b0:b1, :]
+                src = four[:, :, b0:b1].rearrange("p t n -> p n t")
             else:
-                shares = ((0, 0, UB, False), (1, 0, UB - R_V_COLS, False), (1, UB - R_V_COLS, UB, True))
-            for c, b0, b1, on_vector in shares:
-                dst = gh[:, c, b0:b1, :].rearrange("p (n i) t -> p n t i", i=4)
-                four = ztas[g][:, 0:4, :] if c == 0 else ztbs[g][:]
-                src = four[:, :, h * UB + b0 : h * UB + b1].rearrange("p t (n i) -> p n t i", i=4)
-                if on_vector:
-                    nc.vector.tensor_scalar(out=dst, in0=src, scalar1=0.0, scalar2=None, op0=ALU.max)
-                else:
-                    nc.scalar.activation(out=dst, in_=src, func=ACT.Relu)
+                dst = ghs[v][:, c, b0:b1, :].rearrange("p (n i) t -> p n t i", i=4)
+                src = four[:, :, b0:b1].rearrange("p t (n i) -> p n t i", i=4)
+            if engine == "V":
+                nc.vector.tensor_scalar(out=dst, in0=src, scalar1=0.0, scalar2=None, op0=ALU.max)
+            elif engine == "G":
+                nc.gpsimd.tensor_scalar(
+                    out=dst, in0=src, scalar1=1.0, scalar2=0.0, op0=ALU.mult, op1=ALU.add
+                )
+            else:
+                nc.scalar.activation(out=dst, in_=src, func=ACT.Relu)
 
-        def quant(u):
+        def quant(v):
             cd = cod.tile([P, 2 * UB], U32, tag="cd", name="cd", align_bytes=64)
             sc = cod.tile([P, 2 * UB], U8, tag="sc", name="sc", align_bytes=64)
-            cds[u] = cd
-            scs[u] = sc
+            cds[v] = cd
+            scs[v] = sc
             nc.vector.quantize_mx(
                 out=cd[:].bitcast(FP8X4),
                 scales=sc[:],
-                in_=ghs[u][:].rearrange("p c b t -> p (c b t)"),
+                in_=ghs[v][:].rearrange("p c b t -> p (c b t)"),
             )
 
-        def mx(u, tiles):
-            for jj in tiles:
-                acc = psum.tile([P, C], F32, tag="ps", name="acc")
-                accs[(u, jj)] = acc
-                for c in range(2):
-                    col = c * UB + jj * P
-                    nc.tensor.matmul_mx(
-                        out=acc[:],
-                        lhsT=cds[u][:, col : col + P].bitcast(FP8X4),
-                        lhsT_scale=scs[u][:, col : col + P],
-                        rhs=wcodes[:, c * C : (c + 1) * C].bitcast(FP8X4),
-                        rhs_scale=wscl[:, c * C : (c + 1) * C],
-                        start=(c == 0),
-                        stop=(c == 1),
-                    )
+        def mx(v, jj):
+            acc = psa.tile([P, C], F32, tag="acc", name="acc")
+            accs[(v, jj)] = acc
+            for c in range(2):
+                col = c * UB + jj * P
+                nc.tensor.matmul_mx(
+                    out=acc[:],
+                    lhsT=cds[v][:, col : col + P].bitcast(FP8X4),
+                    lhsT_scale=scs[v][:, col : col + P],
+                    rhs=wcodes[:, c * C : (c + 1) * C].bitcast(FP8X4),
+                    rhs_scale=wscl[:, c * C : (c + 1) * C],
+                    start=(c == 0),
+                    stop=(c == 1),
+                )
 
-        def add_bias(u, tiles):
-            g, h = divmod(u, 2)
-            if h == 0 and tiles[0] == 0:
+        def add_bias(v, jj):
+            g, h = divmod(v, 2)
+            if h == 0 and jj == 0:
                 lts[g] = big.tile([P, J, C], F32, tag="big", name="lt", align_bytes=64)
                 negs[g] = small.tile([P, J], F32, name="neg_m")
                 esums[g] = small.tile([P, J], F32, name="esum")
-            lt = lts[g]
-            for jj in tiles:
-                nc.vector.tensor_tensor(
-                    out=lt[:, h * JH + jj, :], in0=accs[(u, jj)][:], in1=bias_bc[:], op=ALU.add
-                )
+            nc.vector.tensor_tensor(
+                out=lts[g][:, h * JH + jj, :], in0=accs[(v, jj)][:], in1=bias_bc[:], op=ALU.add
+            )
 
-        def row_max(u, jj0, jj1):
-            g, h = divmod(u, 2)
+        def row_max(v, jj0, jj1):
+            g, h = divmod(v, 2)
             nc.vector.tensor_reduce(
                 out=negs[g][:, h * JH + jj0 : h * JH + jj1],
                 in_=lts[g][:, h * JH + jj0 : h * JH + jj1, :],
@@ -351,8 +444,8 @@ def tile_binarymlp_pb_t_kernel(tc, z2, g2, beta2, W3, b3, out):
                 negate=True,
             )
 
-        def expsum(u):
-            g, h = divmod(u, 2)
+        def expsum(v):
+            g, h = divmod(v, 2)
             for jj in range(JH):
                 j = h * JH + jj
                 nc.scalar.activation(
@@ -364,70 +457,52 @@ def tile_binarymlp_pb_t_kernel(tc, z2, g2, beta2, W3, b3, out):
                     accum_out=esums[g][:, j : j + 1],
                 )
 
-        def ln_guess(g, j0, j1):
-            n = j1 - j0
-            r_pos = small.tile([P, J], F32, name="r_pos")
-            nc.gpsimd.tensor_tensor(
-                out=r_pos[:, 0:n], in0=esums[g][:, j0:j1], in1=pe_pos[:, 0:n], op=ALU.pow
-            )
-            r_neg = small.tile([P, J], F32, name="r_neg")
-            nc.gpsimd.tensor_tensor(
-                out=r_neg[:, 0:n], in0=esums[g][:, j0:j1], in1=pe_neg[:, 0:n], op=ALU.pow
-            )
+        def ln_pow(g):
+            rpos[g] = small.tile([P, J], F32, name="r_pos")
+            nc.gpsimd.tensor_tensor(out=rpos[g][:], in0=esums[g][:], in1=pe_pos[:], op=ALU.pow)
+
+        def ln_recip(g):
+            rneg[g] = small.tile([P, J], F32, name="r_neg")
+            nc.vector.reciprocal(out=rneg[g][:], in_=rpos[g][:])
+
+        def ln_guess(g):
             t = small.tile([P, J], F32, name="t")
-            lnt[(g, j0)] = t
-            nc.gpsimd.tensor_tensor(
-                out=t[:, 0:n], in0=r_pos[:, 0:n], in1=r_neg[:, 0:n], op=ALU.subtract
-            )
+            lnt[g] = t
+            nc.gpsimd.tensor_tensor(out=t[:], in0=rpos[g][:], in1=rneg[g][:], op=ALU.subtract)
             q = small.tile([P, J], F32, name="q")
             nc.gpsimd.tensor_scalar(
-                out=q[:, 0:n],
-                in0=t[:, 0:n],
-                scalar1=-0.5 * ROOT,
-                scalar2=1.0,
-                op0=ALU.mult,
-                op1=ALU.add,
+                out=q[:], in0=t[:], scalar1=-0.5 * ROOT, scalar2=1.0, op0=ALU.mult, op1=ALU.add
             )
             q2 = small.tile([P, J], F32, name="q2")
-            lnq[(g, j0)] = q2
-            nc.gpsimd.tensor_tensor(
-                out=q2[:, 0:n], in0=q[:, 0:n], in1=negs[g][:, j0:j1], op=ALU.add
-            )
+            lnq[g] = q2
+            nc.gpsimd.tensor_tensor(out=q2[:], in0=q[:], in1=negs[g][:], op=ALU.add)
 
-        def ln_step(g, j0, j1):
-            n = j1 - j0
+        def ln_exp(g):
             e = small.tile([P, J], F32, name="e")
-            nc.scalar.activation(
-                out=e[:, 0:n], in_=lnt[(g, j0)][:, 0:n], func=ACT.Exp, scale=-0.5 * ROOT
-            )
+            lne[g] = e
+            nc.scalar.activation(out=e[:], in_=lnt[g][:], func=ACT.Exp, scale=-0.5 * ROOT)
+
+        def ln_step(g):
             w = small.tile([P, J], F32, name="w")
-            nc.gpsimd.tensor_tensor(
-                out=w[:, 0:n], in0=esums[g][:, j0:j1], in1=e[:, 0:n], op=ALU.mult
-            )
-            neg_c = small.tile([P, J], F32, name="neg_c")
-            shifts[(g, j0)] = neg_c
-            nc.gpsimd.tensor_tensor(
-                out=neg_c[:, 0:n], in0=lnq[(g, j0)][:, 0:n], in1=w[:, 0:n], op=ALU.subtract
-            )
+            nc.gpsimd.tensor_tensor(out=w[:], in0=esums[g][:], in1=lne[g][:], op=ALU.mult)
+            shifts[g] = small.tile([P, J], F32, name="neg_c")
+            nc.gpsimd.tensor_tensor(out=shifts[g][:], in0=lnq[g][:], in1=w[:], op=ALU.subtract)
 
-        def ln_table(g, j0, j1):
+        def ln_table(g):
             y = small.tile([P, J], F32, name="y")
-            lne[(g, j0)] = y
-            nc.scalar.activation(out=y[:, 0 : j1 - j0], in_=esums[g][:, j0:j1], func=ACT.Ln)
+            lne[g] = y
+            nc.scalar.activation(out=y[:], in_=esums[g][:], func=ACT.Ln)
 
-        def ln_table_shift(g, j0, j1):
-            n = j1 - j0
-            neg_c = small.tile([P, J], F32, name="neg_c")
-            shifts[(g, j0)] = neg_c
-            nc.vector.tensor_tensor(
-                out=neg_c[:, 0:n], in0=negs[g][:, j0:j1], in1=lne[(g, j0)][:, 0:n], op=ALU.subtract
-            )
+        def ln_table_shift(g):
+            shifts[g] = small.tile([P, J], F32, name="neg_c")
+            nc.vector.tensor_tensor(out=shifts[g][:], in0=negs[g][:], in1=lne[g][:], op=ALU.subtract)
 
-        def subtract_store(g, h, key, engines):
+        def subtract_store(v, engines):
+            g, h = divmod(v, 2)
             lt = lts[g]
             for jj in range(JH):
                 j = h * JH + jj
-                shift = shifts[key][:, j - key[1] : j - key[1] + 1]
+                shift = shifts[g][:, j : j + 1]
                 engine = engines[jj]
                 if engine == "V":
                     nc.vector.tensor_scalar(
@@ -435,71 +510,99 @@ def tile_binarymlp_pb_t_kernel(tc, z2, g2, beta2, W3, b3, out):
                     )
                 elif engine == "G":
                     nc.gpsimd.tensor_scalar(
-                        out=lt[:, j, :],
-                        in0=lt[:, j, :],
-                        scalar1=1.0,
-                        scalar2=shift,
-                        op0=ALU.mult,
-                        op1=ALU.add,
+                        out=lt[:, j, :], in0=lt[:, j, :], scalar1=1.0, scalar2=shift, op0=ALU.mult, op1=ALU.add
                     )
                 else:
                     nc.scalar.activation(
                         out=lt[:, j, :], in_=lt[:, j, :], func=ACT.Identity, bias=shift, scale=1.0
                     )
-            u = 2 * g + h
             nc.sync.dma_start(
-                out=out[u * UB : (u + 1) * UB, :].rearrange("(p j) c -> p j c", j=JH),
+                out=out[v * UB : (v + 1) * UB, :].rearrange("(p j) c -> p j c", j=JH),
                 in_=lt[:, h * JH : (h + 1) * JH, :],
             )
 
-        affine(0, 0)
-        affine(0, 1)
-        regroup(0)
-        regroup(1)
-        nc.vector.quantize_mx(
-            out=wcodes[:].bitcast(FP8X4),
-            scales=wscl[:],
-            in_=gw[:].rearrange("p c n t -> p (c n t)"),
-        )
+        affine_s(0)
+        for t in range(4):
+            affine_v(0, t)
+            if t < 2:
+                late_tile(0, t + 2)
+                late_words(1, t)
+            else:
+                late_tile(1, t - 2)
+        regroup(0, 0, 0, UB, "V")
+        regroup(0, 1, 0, UB, "V")
+        affine_s(1)
+        late_words(2, 0)
+        late_words(2, 1)
+        regroup(1, 1, 0, UB, "G")
+        regroup(1, 0, 0, UB, "S")
         quant(0)
-        mx(0, range(JH))
-        affine(1, 0)
-        affine(1, 1)
-        for v in range(U + 1):
-            if v + 1 < U:
-                quant(v + 1)
-            if v < U - 1:
-                for jj in range(JH):
-                    add_bias(v, range(jj, jj + 1))
-                    mx(v + 1, range(jj, jj + 1))
-            if v % 2 == 0 and v + 4 < U:
-                late_transposes((v + 4) // 2)
-            if v == U - 1:
-                for jj in range(JH):
-                    add_bias(v, range(jj, jj + 1))
-                    if jj >= 1:
-                        row_max(v, jj - 1, jj)
-                row_max(v, JH - 1, JH)
+        for t in range(4):
+            mx(0, t)
+            affine_v(1, t)
+            late_tile(1 if t < 2 else 2, (t + 2) % 4)
+        affine_s(2)
+        late_words(3, 0)
+        late_words(3, 1)
+        for v in range(U - 2):
+            g_a, t_a = (v + 4) // 2, 2 * (v % 2)
+            g_t, t_t = (v + 5) // 2, 2 * ((v + 1) % 2)
+            g_p = (v - 3) // 2 if v % 2 == 1 and v >= 3 else -1
+            g_l = (v - 4) // 2 if v % 2 == 0 and v >= 4 else -1
+            if v + 3 < U:
+                affine_s(v + 3)
+            regroup(v + 2, 1, 0, UB, "G")
+            regroup(v + 2, 0, 0, UB, "S")
+            quant(v + 1)
+            if g_p >= 0:
+                ln_pow(g_p)
+            if g_l >= 0:
+                ln_guess(g_l)
+                ln_exp(g_l)
+            for jj in range(JH):
+                add_bias(v, jj)
+                mx(v + 1, jj)
+                if jj < 2:
+                    if g_a < G:
+                        affine_v(g_a, t_a + jj)
+                    if g_t < G:
+                        late_tile(g_t, t_t + jj)
+                elif v + 4 < U:
+                    late_words(v + 4, jj - 2)
+            if g_p >= 0:
+                ln_recip(g_p)
+            row_max(v, 0, JH)
             if v >= 1:
                 expsum(v - 1)
-            gf, odd = divmod(v - 2, 2)
-            if v >= 2 and odd == 0 and gf < G - 1:
-                ln_guess(gf, 0, J)
-            if v >= 3 and odd == 1:
-                ln_step(gf, 0, J)
-            if v == U:
-                ln_table(G - 1, 0, J)
-            if v + 2 < U:
-                regroup(v + 2)
-            if v + 4 < U:
-                affine((v + 4) // 2, v % 2)
-            if v < U - 1:
-                row_max(v, 0, JH)
-            if v >= 3 and odd == 1:
-                subtract_store(gf, 0, (gf, 0), "GGGG" if v < U - 2 else "SSSS")
-            if v >= 4 and odd == 0:
-                subtract_store(gf - 1, 1, (gf - 1, 0), "GGGG" if v < U - 2 else "VVVV")
-            if v == U:
-                ln_table_shift(G - 1, 0, J)
-                subtract_store(G - 1, 0, (G - 1, 0), "VVVV")
-                subtract_store(G - 1, 1, (G - 1, 0), "SSVV")
+            if v >= 5:
+                subtract_store(v - 5, "GGGG" if v < U - 4 else "GGVV")
+            if g_l >= 0:
+                ln_step(g_l)
+        quant(U - 1)
+        ln_guess(G - 3)
+        ln_exp(G - 3)
+        ln_step(G - 3)
+        expsum(U - 3)
+        ln_pow(G - 2)
+        for jj in range(JH):
+            add_bias(U - 2, jj)
+            mx(U - 1, jj)
+        row_max(U - 2, 0, JH)
+        ln_recip(G - 2)
+        subtract_store(U - 7, "SSSV")
+        ln_guess(G - 2)
+        ln_exp(G - 2)
+        ln_step(G - 2)
+        expsum(U - 2)
+        for jj in range(JH):
+            add_bias(U - 1, jj)
+            row_max(U - 1, jj, jj + 1)
+        subtract_store(U - 6, "GGVV")
+        subtract_store(U - 5, "GGVV")
+        expsum(U - 1)
+        subtract_store(U - 4, "VVVV")
+        subtract_store(U - 3, "VVVV")
+        ln_table(G - 1)
+        ln_table_shift(G - 1)
+        subtract_store(U - 2, "VVVV")
+        subtract_store(U - 1, "SSVV")

@@ -28,6 +28,7 @@ J = GB // P
 BN_EPS = 1e-5
 ROOT = 1024.0
 N_WARM = 12
+N_KEEP = 6
 G_W = 1
 G_WT = 3
 CHUNK = 256
@@ -409,6 +410,19 @@ def tile_binarymlp_pb_t_kernel(tc, z2, g2, beta2, W3, b3, out):
                 in_=ghs[v][:].rearrange("p c b t -> p (c b t)"),
             )
 
+        def keep_warm(n):
+            pk = psa.tile([P, C], F32, tag="acc", name="pk")
+            for i in range(n):
+                nc.tensor.matmul_mx(
+                    out=pk[:],
+                    lhsT=wcodes[:, 0:P].bitcast(FP8X4),
+                    lhsT_scale=wscl[:, 0:P],
+                    rhs=wcodes[:, 0:C].bitcast(FP8X4),
+                    rhs_scale=wscl[:, 0:C],
+                    start=True,
+                    stop=True,
+                )
+
         def mx(v, jj):
             acc = psa.tile([P, C], F32, tag="acc", name="acc")
             accs[(v, jj)] = acc
@@ -537,13 +551,16 @@ def tile_binarymlp_pb_t_kernel(tc, z2, g2, beta2, W3, b3, out):
         regroup(1, 1, 0, UB, "G")
         regroup(1, 0, 0, UB, "S")
         quant(0)
+        keep_warm(N_KEEP)
+        for jj in range(JH):
+            mx(0, jj)
         for t in range(4):
-            mx(0, t)
             affine_v(1, t)
             late_tile(1 if t < 2 else 2, (t + 2) % 4)
         affine_s(2)
         late_words(3, 0)
         late_words(3, 1)
+        quant(1)
         for v in range(U - 2):
             g_a, t_a = (v + 4) // 2, 2 * (v % 2)
             g_t, t_t = (v + 5) // 2, 2 * ((v + 1) % 2)
@@ -553,7 +570,6 @@ def tile_binarymlp_pb_t_kernel(tc, z2, g2, beta2, W3, b3, out):
                 affine_s(v + 3)
             regroup(v + 2, 1, 0, UB, "G")
             regroup(v + 2, 0, 0, UB, "S")
-            quant(v + 1)
             if g_p >= 0:
                 ln_pow(g_p)
             if g_l >= 0:
@@ -562,6 +578,10 @@ def tile_binarymlp_pb_t_kernel(tc, z2, g2, beta2, W3, b3, out):
             for jj in range(JH):
                 add_bias(v, jj)
                 mx(v + 1, jj)
+                if jj > 0:
+                    row_max(v, jj - 1, jj)
+                elif v >= 1:
+                    row_max(v - 1, JH - 1, JH)
                 if jj < 2:
                     if g_a < G:
                         affine_v(g_a, t_a + jj)
@@ -569,25 +589,29 @@ def tile_binarymlp_pb_t_kernel(tc, z2, g2, beta2, W3, b3, out):
                         late_tile(g_t, t_t + jj)
                 elif v + 4 < U:
                     late_words(v + 4, jj - 2)
+                if jj == 2:
+                    quant(v + 2)
             if g_p >= 0:
                 ln_recip(g_p)
-            row_max(v, 0, JH)
             if v >= 1:
                 expsum(v - 1)
             if v >= 5:
                 subtract_store(v - 5, "GGGG" if v < U - 4 else "GGVV")
             if g_l >= 0:
                 ln_step(g_l)
-        quant(U - 1)
         ln_guess(G - 3)
         ln_exp(G - 3)
         ln_step(G - 3)
-        expsum(U - 3)
-        ln_pow(G - 2)
         for jj in range(JH):
             add_bias(U - 2, jj)
             mx(U - 1, jj)
-        row_max(U - 2, 0, JH)
+            if jj == 0:
+                row_max(U - 3, JH - 1, JH)
+                expsum(U - 3)
+                ln_pow(G - 2)
+            else:
+                row_max(U - 2, jj - 1, jj)
+        row_max(U - 2, JH - 1, JH)
         ln_recip(G - 2)
         subtract_store(U - 7, "SSSV")
         ln_guess(G - 2)

@@ -102,7 +102,7 @@ def tile_binarymlp_pb_t_kernel(tc, z2, g2, beta2, W3, b3, out):
         rows = const.tile([P, PASS_K], F32, name="rows", align_bytes=64)
         nc.gpsimd.memset(rows[:], 0.0)
         stat = const.tile([P, 2 * KT], F32, name="stat")
-        junk_s = const.tile([P, GB], BF16, name="junk_s")
+        junk_s = const.tile([P, UB], BF16, name="junk_s")
         junk_e = const.tile([P, C], BF16, name="junk_e")
         junk_d = const.tile([P, P], F32, name="junk_d")
         gb = const.tile([P, 2 * KT], F32, name="gb")
@@ -121,7 +121,7 @@ def tile_binarymlp_pb_t_kernel(tc, z2, g2, beta2, W3, b3, out):
         grams = []
         for i in range(NG):
             grams.append(psa.tile([P, P], F32, tag="acc", name="gram%d" % i))
-        psums = psa.tile([P, 6 * G], F32, tag="acc", name="psums")
+        psums = psa.tile([P, 4 * U + 2 * G], F32, tag="acc", name="psums")
         plain = [(0, 0), (0, 1), (1, 0), (1, 1)]
         cols = [c * PASS_K + 256 + h * P for c, h in plain]
         n_v = [0, NCH]
@@ -159,30 +159,54 @@ def tile_binarymlp_pb_t_kernel(tc, z2, g2, beta2, W3, b3, out):
             zw = zn[:].bitcast(F32)
             for h in range(2):
                 u = 2 * g + h
-                if h == 0:
-                    pt = pst.tile([P, GB], BF16, tag="tr", name="pt")
+                js = range(h * JH, (h + 1) * JH)
+                pws = []
                 for c in range(2):
                     pw2 = pst.tile([P, JH * P], F32, tag="tr", name="pw2")
+                    pws.append(pw2[:].bitcast(BF16))
                     for j in range(JH):
                         nc.tensor.transpose(
                             pw2[:, j * P : (j + 1) * P], zw[:, h * JH + j, 256 * c : 256 * c + P], identf[:]
                         )
-                    for i in range(NG):
-                        for j in range(2 * c, 2 * c + 2):
-                            jj = h * JH + j
+                pt = pst.tile([P, UB], BF16, tag="tr", name="pt")
+                for j in range(JH):
+                    nc.tensor.transpose(
+                        pt[:, j * P : (j + 1) * P], zn[:, h * JH + j, cols[3] : cols[3] + P], ident[:]
+                    )
+                for i in range(NG):
+                    for j in js:
+                        nc.tensor.matmul(
+                            out=grams[i][:],
+                            lhsT=zn[:, j, cols[i] : cols[i] + P],
+                            rhs=zn[:, j, cols[i] : cols[i] + P],
+                            start=(g == 0 and j == 0),
+                            stop=(g == G - 1 and j == J - 1),
+                        )
+                for i in range(4):
+                    for j in js:
+                        nc.tensor.matmul(
+                            out=psums[:, i * U + u : i * U + u + 1],
+                            lhsT=zn[:, j, cols[i] : cols[i] + P],
+                            rhs=inv_col[:],
+                            start=(j == js[0]),
+                            stop=(j == js[-1]),
+                        )
+                if h == 0:
+                    for e in range(2):
+                        for j in js:
                             nc.tensor.matmul(
-                                out=grams[i][:],
-                                lhsT=zn[:, jj, cols[i] : cols[i] + P],
-                                rhs=zn[:, jj, cols[i] : cols[i] + P],
-                                start=(g == 0 and jj == 0),
-                                stop=(g == G - 1 and jj == J - 1),
+                                out=psums[:, 4 * U + e * G + g : 4 * U + e * G + g + 1],
+                                lhsT=zn[:, j, PASS_K + e : PASS_K + 256 : 2],
+                                rhs=inv_col[:],
+                                start=(j == js[0]),
+                                stop=(j == js[-1]),
                             )
-                    pb2 = pw2[:].bitcast(BF16)
+                for c in range(2):
                     if c == 1 and h == 0:
                         for e in range(2):
                             nc.scalar.activation(
-                                out=junk_s[:, 0:UB],
-                                in_=pb2[:, e : 2 * UB : 2],
+                                out=junk_s[:],
+                                in_=pws[c][:, e : 2 * UB : 2],
                                 func=ACT.Square,
                                 accum_out=qsum[:, e, NV + g : NV + g + 1],
                             )
@@ -190,34 +214,8 @@ def tile_binarymlp_pb_t_kernel(tc, z2, g2, beta2, W3, b3, out):
                         for q in range(2):
                             n = n_v[c] * 6
                             n_v[c] += 1
-                            nc.vector.bn_stats(out=bs[:, n : n + 6], in_=pb2[:, q * 512 : (q + 1) * 512])
-                for j in range(h * JH, (h + 1) * JH):
-                    nc.tensor.transpose(pt[:, j * P : (j + 1) * P], zn[:, j, cols[3] : cols[3] + P], ident[:])
-                nc.scalar.activation(
-                    out=junk_s[:, 0:UB],
-                    in_=pt[:, h * UB : (h + 1) * UB],
-                    func=ACT.Square,
-                    accum_out=sq[:, u : u + 1],
-                )
-                if h == 0:
-                    for e in range(2):
-                        for j in range(JH):
-                            nc.tensor.matmul(
-                                out=psums[:, (4 + e) * G + g : (4 + e) * G + g + 1],
-                                lhsT=zn[:, j, PASS_K + e : PASS_K + 256 : 2],
-                                rhs=inv_col[:],
-                                start=(j == 0),
-                                stop=(j == JH - 1),
-                            )
-            for i in range(4):
-                for j in range(J):
-                    nc.tensor.matmul(
-                        out=psums[:, i * G + g : i * G + g + 1],
-                        lhsT=zn[:, j, cols[i] : cols[i] + P],
-                        rhs=inv_col[:],
-                        start=(j == 0),
-                        stop=(j == J - 1),
-                    )
+                            nc.vector.bn_stats(out=bs[:, n : n + 6], in_=pws[c][:, q * 512 : (q + 1) * 512])
+                nc.scalar.activation(out=junk_s[:], in_=pt[:], func=ACT.Square, accum_out=sq[:, u : u + 1])
             if g >= G_WT and g < G_WT + 4:
                 w_bank(g - G_WT)
             if g == G_WT + 3:
@@ -256,7 +254,7 @@ def tile_binarymlp_pb_t_kernel(tc, z2, g2, beta2, W3, b3, out):
         mean_v = bsv[:, :, 0:NV, 1]
         nc.vector.tensor_reduce(
             out=bsv[:, :, NV, 1],
-            in_=psums[:, 4 * G : 6 * G].rearrange("p (e g) -> p e g", e=2),
+            in_=psums[:, 4 * U : 4 * U + 2 * G].rearrange("p (e g) -> p e g", e=2),
             axis=AX.X,
             op=ALU.add,
         )
@@ -288,7 +286,7 @@ def tile_binarymlp_pb_t_kernel(tc, z2, g2, beta2, W3, b3, out):
             nc.vector.tensor_reduce(out=abv[:, 0, :, 2 + c], in_=qsum[:, :, n0:n1], axis=AX.X, op=ALU.add)
         nc.vector.tensor_reduce(
             out=abv[:, 1, :, 0:2],
-            in_=psums[:, 0 : 4 * G].rearrange("p (c h g) -> p h c g", c=2, h=2),
+            in_=psums[:, 0 : 4 * U].rearrange("p (c h u) -> p h c u", c=2, h=2),
             axis=AX.X,
             op=ALU.add,
         )
@@ -324,6 +322,7 @@ def tile_binarymlp_pb_t_kernel(tc, z2, g2, beta2, W3, b3, out):
         sd = const.tile([P, KT], F32, name="sd")
         nc.scalar.activation(out=sd[:], in_=ve[:], func=ACT.Sqrt)
         nc.scalar.activation(out=warm[:], in_=one[:], func=ACT.Exp)
+        nc.scalar.activation(out=warm[:], in_=one[:], func=ACT.Relu, bias=one[:], scale=one[:])
         mean = const.tile([P, KT], F32, name="mean")
         nc.vector.tensor_scalar(
             out=mean[:], in0=ssum, scalar1=float(CHUNK) / B, scalar2=None, op0=ALU.mult

@@ -322,7 +322,6 @@ def tile_binarymlp_pb_t_kernel(tc, z2, g2, beta2, W3, b3, out):
         sd = const.tile([P, KT], F32, name="sd")
         nc.scalar.activation(out=sd[:], in_=ve[:], func=ACT.Sqrt)
         nc.scalar.activation(out=warm[:], in_=one[:], func=ACT.Exp)
-        nc.scalar.activation(out=warm[:], in_=one[:], func=ACT.Relu, bias=one[:], scale=one[:])
         mean = const.tile([P, KT], F32, name="mean")
         nc.vector.tensor_scalar(
             out=mean[:], in0=ssum, scalar1=float(CHUNK) / B, scalar2=None, op0=ALU.mult
@@ -595,7 +594,7 @@ def tile_binarymlp_pb_t_kernel(tc, z2, g2, beta2, W3, b3, out):
             if v >= 1:
                 expsum(v - 1)
             if v >= 5:
-                subtract_store(v - 5, "GGGG" if v < U - 4 else "GGVV")
+                subtract_store(v - 5, "GGVV")
             if g_l >= 0:
                 ln_step(g_l)
         ln_guess(G - 3)

@@ -28,12 +28,15 @@ J = GB // P
 BN_EPS = 1e-5
 ROOT = 1024.0
 N_WARM = 12
+G_PIECE = 512
 N_KEEP = 6
 G_W = 1
 G_WT = 3
 CHUNK = 256
 NCH = B // CHUNK
-NV = NCH + NCH // 2
+S_GROUPS = tuple(range(1, G, 2))
+NS = len(S_GROUPS)
+NV = 2 * NCH - 2 * NS
 INV = 1.0 / CHUNK
 NG = 3
 
@@ -95,16 +98,16 @@ def tile_binarymlp_pb_t_kernel(tc, z2, g2, beta2, W3, b3, out):
 
         bs = const.tile([P, (NV + 1) * 6], F32, name="bs")
         msq = const.tile([P, 2 * NV], F32, name="msq")
-        qsum = const.tile([P, 2, NV + G], F32, name="qsum")
+        qsum = const.tile([P, 2, NV + NS], F32, name="qsum")
         sq = const.tile([P, U], F32, name="sq")
         ab = const.tile([P, 4 * P], F32, name="ab", align_bytes=64)
         nc.gpsimd.memset(ab[:], 0.0)
         rows = const.tile([P, PASS_K], F32, name="rows", align_bytes=64)
         nc.gpsimd.memset(rows[:], 0.0)
         stat = const.tile([P, 2 * KT], F32, name="stat")
-        junk_s = const.tile([P, UB], BF16, name="junk_s")
-        junk_e = const.tile([P, C], BF16, name="junk_e")
-        junk_d = const.tile([P, P], F32, name="junk_d")
+        junk_s = const.tile([P, 3, UB], BF16, name="junk_s")
+        junk_e = const.tile([P, JH, C], BF16, name="junk_e")
+        junk_d = const.tile([P, NG, P], F32, name="junk_d")
         gb = const.tile([P, 2 * KT], F32, name="gb")
         bias_bc = const.tile([P, C], F32, name="bias_bc")
 
@@ -121,7 +124,7 @@ def tile_binarymlp_pb_t_kernel(tc, z2, g2, beta2, W3, b3, out):
         grams = []
         for i in range(NG):
             grams.append(psa.tile([P, P], F32, tag="acc", name="gram%d" % i))
-        psums = psa.tile([P, 4 * U + 2 * G], F32, tag="acc", name="psums")
+        psums = psa.tile([P, 4 * U + 2 * NS], F32, tag="acc", name="psums")
         plain = [(0, 0), (0, 1), (1, 0), (1, 1)]
         cols = [c * PASS_K + 256 + h * P for c, h in plain]
         n_v = [0, NCH]
@@ -191,31 +194,33 @@ def tile_binarymlp_pb_t_kernel(tc, z2, g2, beta2, W3, b3, out):
                             start=(j == js[0]),
                             stop=(j == js[-1]),
                         )
-                if h == 0:
+                on_scalar = h == 0 and g in S_GROUPS
+                if on_scalar:
+                    s_col = S_GROUPS.index(g)
                     for e in range(2):
                         for j in js:
                             nc.tensor.matmul(
-                                out=psums[:, 4 * U + e * G + g : 4 * U + e * G + g + 1],
+                                out=psums[:, 4 * U + e * NS + s_col : 4 * U + e * NS + s_col + 1],
                                 lhsT=zn[:, j, PASS_K + e : PASS_K + 256 : 2],
                                 rhs=inv_col[:],
                                 start=(j == js[0]),
                                 stop=(j == js[-1]),
                             )
                 for c in range(2):
-                    if c == 1 and h == 0:
+                    if c == 1 and on_scalar:
                         for e in range(2):
                             nc.scalar.activation(
-                                out=junk_s[:],
+                                out=junk_s[:, e, :],
                                 in_=pws[c][:, e : 2 * UB : 2],
                                 func=ACT.Square,
-                                accum_out=qsum[:, e, NV + g : NV + g + 1],
+                                accum_out=qsum[:, e, NV + s_col : NV + s_col + 1],
                             )
                     else:
                         for q in range(2):
                             n = n_v[c] * 6
                             n_v[c] += 1
                             nc.vector.bn_stats(out=bs[:, n : n + 6], in_=pws[c][:, q * 512 : (q + 1) * 512])
-                nc.scalar.activation(out=junk_s[:], in_=pt[:], func=ACT.Square, accum_out=sq[:, u : u + 1])
+                nc.scalar.activation(out=junk_s[:, 2, :], in_=pt[:], func=ACT.Square, accum_out=sq[:, u : u + 1])
             if g >= G_WT and g < G_WT + 4:
                 w_bank(g - G_WT)
             if g == G_WT + 3:
@@ -228,8 +233,11 @@ def tile_binarymlp_pb_t_kernel(tc, z2, g2, beta2, W3, b3, out):
         dts = {}
         wts = {}
 
-        def late_tile(g, t):
-            dt = pst.tile([P, GB], BF16, tag="tr", name="dt")
+        def late_tile(g, t, early=False):
+            if early:
+                dt = psa.tile([P, GB], BF16, tag="acc", name="dte")
+            else:
+                dt = pst.tile([P, GB], BF16, tag="tr", name="dt")
             dts[(g, t)] = dt
             for j in range(J):
                 nc.tensor.transpose(dt[:, j * P : (j + 1) * P], zns[g][:, j, t:PASS_K:4], ident[:])
@@ -254,7 +262,7 @@ def tile_binarymlp_pb_t_kernel(tc, z2, g2, beta2, W3, b3, out):
         mean_v = bsv[:, :, 0:NV, 1]
         nc.vector.tensor_reduce(
             out=bsv[:, :, NV, 1],
-            in_=psums[:, 4 * U : 4 * U + 2 * G].rearrange("p (e g) -> p e g", e=2),
+            in_=psums[:, 4 * U : 4 * U + 2 * NS].rearrange("p (e g) -> p e g", e=2),
             axis=AX.X,
             op=ALU.add,
         )
@@ -274,7 +282,7 @@ def tile_binarymlp_pb_t_kernel(tc, z2, g2, beta2, W3, b3, out):
         for i in range(NG):
             c, h = plain[i]
             nc.vector.scalar_tensor_tensor(
-                out=junk_d[:],
+                out=junk_d[:, i, :],
                 in0=grams[i][:],
                 scalar=1.0,
                 in1=ident[:],
@@ -282,7 +290,7 @@ def tile_binarymlp_pb_t_kernel(tc, z2, g2, beta2, W3, b3, out):
                 op1=ALU.mult,
                 accum_out=abv[:, 1, h, 2 + c : 3 + c],
             )
-        for c, n0, n1 in ((0, 0, NCH), (1, NCH, NV + G)):
+        for c, n0, n1 in ((0, 0, NCH), (1, NCH, NV + NS)):
             nc.vector.tensor_reduce(out=abv[:, 0, :, 2 + c], in_=qsum[:, :, n0:n1], axis=AX.X, op=ALU.add)
         nc.vector.tensor_reduce(
             out=abv[:, 1, :, 0:2],
@@ -294,17 +302,23 @@ def tile_binarymlp_pb_t_kernel(tc, z2, g2, beta2, W3, b3, out):
         pt1 = psa.tile([P, 4 * P], F32, tag="acc", name="pt1")
         for q in range(4):
             nc.tensor.transpose(pt1[:, q * P : (q + 1) * P], ab[:, q * P : (q + 1) * P], identf[:])
+        rows_v = rows[0:4, :].rearrange("r (t p) -> r t p", t=4)
+        for e in range(2):
+            nc.vector.tensor_copy(
+                out=rows_v[:, e:4:2, 0:64],
+                in_=pt1[0:4, e * P : (e + 1) * P].rearrange("r (p d) -> r d p", d=2),
+            )
         nc.vector.tensor_copy(
-            out=rows[0:4, 0:256].rearrange("r (q e) -> r q e", e=2),
-            in_=pt1[0:4, 0:256].rearrange("r (e q) -> r q e", e=2),
+            out=rows_v[:, :, 64:P], in_=pt1[0:4, 256:512].rearrange("r (p t) -> r t p", t=4)
         )
-        nc.vector.tensor_copy(out=rows[0:4, 256:512], in_=pt1[0:4, 256:512])
         pt2 = psa.tile([P, 4, P], F32, tag="acc", name="pt2")
         for t in range(4):
-            nc.tensor.transpose(pt2[:, t, :], rows[:, t:PASS_K:4], identf[:])
+            nc.tensor.transpose(pt2[:, t, :], rows[:, t * P : (t + 1) * P], identf[:])
         nc.vector.tensor_copy(
             out=stat[:].rearrange("p (r t) -> p r t", t=4), in_=pt2[:, :, 0:4].rearrange("p t r -> p r t")
         )
+        late_tile(0, 2, early=True)
+        late_tile(0, 3, early=True)
         ssum = stat[:, 0:KT]
         ssq = stat[:, KT : 2 * KT]
         m2 = const.tile([P, KT], F32, name="m2")
@@ -347,6 +361,8 @@ def tile_binarymlp_pb_t_kernel(tc, z2, g2, beta2, W3, b3, out):
         lnt = {}
         lne = {}
         lnq = {}
+        lnp = {}
+        lnw = {}
         shifts = {}
         ztas = {}
         zss = {}
@@ -382,18 +398,20 @@ def tile_binarymlp_pb_t_kernel(tc, z2, g2, beta2, W3, b3, out):
             if v not in ghs:
                 ghs[v] = grp.tile([P, 2, UB, 4], BF16, tag="gr", name="gh", align_bytes=64)
             four = ztas[g][:, :, h * UB : (h + 1) * UB] if c == 0 else zss[v][:]
-            if engine == "G":
-                dst = ghs[v][:, c, b0:b1, :]
-                src = four[:, :, b0:b1].rearrange("p t n -> p n t")
-            else:
-                dst = ghs[v][:, c, b0:b1, :].rearrange("p (n i) t -> p n t i", i=4)
-                src = four[:, :, b0:b1].rearrange("p t (n i) -> p n t i", i=4)
+            dst = ghs[v][:, c, b0:b1, :].rearrange("p (n i) t -> p n t i", i=4)
+            src = four[:, :, b0:b1].rearrange("p t (n i) -> p n t i", i=4)
             if engine == "V":
                 nc.vector.tensor_scalar(out=dst, in0=src, scalar1=0.0, scalar2=None, op0=ALU.max)
             elif engine == "G":
-                nc.gpsimd.tensor_scalar(
-                    out=dst, in0=src, scalar1=1.0, scalar2=0.0, op0=ALU.mult, op1=ALU.add
-                )
+                for n in range(b0, b1, G_PIECE):
+                    nc.gpsimd.tensor_scalar(
+                        out=ghs[v][:, c, n : n + G_PIECE, :],
+                        in0=four[:, :, n : n + G_PIECE].rearrange("p t n -> p n t"),
+                        scalar1=1.0,
+                        scalar2=0.0,
+                        op0=ALU.mult,
+                        op1=ALU.add,
+                    )
             else:
                 nc.scalar.activation(out=dst, in_=src, func=ACT.Relu)
 
@@ -456,12 +474,12 @@ def tile_binarymlp_pb_t_kernel(tc, z2, g2, beta2, W3, b3, out):
                 negate=True,
             )
 
-        def expsum(v):
+        def expsum(v, jj0=0, jj1=JH):
             g, h = divmod(v, 2)
-            for jj in range(JH):
+            for jj in range(jj0, jj1):
                 j = h * JH + jj
                 nc.scalar.activation(
-                    out=junk_e[:],
+                    out=junk_e[:, jj, :],
                     in_=lts[g][:, j, :],
                     func=ACT.Exp,
                     bias=negs[g][:, j : j + 1],
@@ -469,52 +487,88 @@ def tile_binarymlp_pb_t_kernel(tc, z2, g2, beta2, W3, b3, out):
                     accum_out=esums[g][:, j : j + 1],
                 )
 
-        def ln_pow(g):
-            rpos[g] = small.tile([P, J], F32, name="r_pos")
-            nc.gpsimd.tensor_tensor(out=rpos[g][:], in0=esums[g][:], in1=pe_pos[:], op=ALU.pow)
-
-        def ln_recip(g):
-            rneg[g] = small.tile([P, J], F32, name="r_neg")
-            nc.vector.reciprocal(out=rneg[g][:], in_=rpos[g][:])
-
-        def ln_guess(g):
-            t = small.tile([P, J], F32, name="t")
-            lnt[g] = t
-            nc.gpsimd.tensor_tensor(out=t[:], in0=rpos[g][:], in1=rneg[g][:], op=ALU.subtract)
-            q = small.tile([P, J], F32, name="q")
-            nc.gpsimd.tensor_scalar(
-                out=q[:], in0=t[:], scalar1=-0.5 * ROOT, scalar2=1.0, op0=ALU.mult, op1=ALU.add
+        def ln_pow(key):
+            g, j0, j1 = key
+            rpos[key] = small.tile([P, J], F32, name="r_pos")
+            nc.gpsimd.tensor_tensor(
+                out=rpos[key][:, j0:j1], in0=esums[g][:, j0:j1], in1=pe_pos[:, j0:j1], op=ALU.pow
             )
-            q2 = small.tile([P, J], F32, name="q2")
-            lnq[g] = q2
-            nc.gpsimd.tensor_tensor(out=q2[:], in0=q[:], in1=negs[g][:], op=ALU.add)
 
-        def ln_exp(g):
-            e = small.tile([P, J], F32, name="e")
-            lne[g] = e
-            nc.scalar.activation(out=e[:], in_=lnt[g][:], func=ACT.Exp, scale=-0.5 * ROOT)
+        def ln_recip(key):
+            g, j0, j1 = key
+            rneg[key] = small.tile([P, J], F32, name="r_neg")
+            nc.vector.reciprocal(out=rneg[key][:, j0:j1], in_=rpos[key][:, j0:j1])
 
-        def ln_step(g):
-            w = small.tile([P, J], F32, name="w")
-            nc.gpsimd.tensor_tensor(out=w[:], in0=esums[g][:], in1=lne[g][:], op=ALU.mult)
-            shifts[g] = small.tile([P, J], F32, name="neg_c")
-            nc.gpsimd.tensor_tensor(out=shifts[g][:], in0=lnq[g][:], in1=w[:], op=ALU.subtract)
+        def ln_diff(key):
+            g, j0, j1 = key
+            lnt[key] = small.tile([P, J], F32, name="t")
+            nc.gpsimd.tensor_tensor(
+                out=lnt[key][:, j0:j1], in0=rpos[key][:, j0:j1], in1=rneg[key][:, j0:j1], op=ALU.subtract
+            )
 
-        def ln_table(g):
+        def ln_exp(key):
+            g, j0, j1 = key
+            lne[key] = small.tile([P, J], F32, name="e")
+            nc.scalar.activation(
+                out=lne[key][:, j0:j1], in_=lnt[key][:, j0:j1], func=ACT.Exp, scale=-0.5 * ROOT
+            )
+
+        def ln_first(key):
+            g, j0, j1 = key
+            lnq[key] = small.tile([P, J], F32, name="q")
+            nc.gpsimd.tensor_scalar(
+                out=lnq[key][:, j0:j1],
+                in0=lnt[key][:, j0:j1],
+                scalar1=-0.5 * ROOT,
+                scalar2=1.0,
+                op0=ALU.mult,
+                op1=ALU.add,
+            )
+
+        def ln_second(key):
+            g, j0, j1 = key
+            lnp[key] = small.tile([P, J], F32, name="q2")
+            nc.gpsimd.tensor_tensor(
+                out=lnp[key][:, j0:j1], in0=lnq[key][:, j0:j1], in1=negs[g][:, j0:j1], op=ALU.add
+            )
+
+        def ln_mul(key):
+            g, j0, j1 = key
+            lnw[key] = small.tile([P, J], F32, name="w")
+            nc.gpsimd.tensor_tensor(
+                out=lnw[key][:, j0:j1], in0=esums[g][:, j0:j1], in1=lne[key][:, j0:j1], op=ALU.mult
+            )
+
+        def ln_shift(key):
+            g, j0, j1 = key
+            neg_c = small.tile([P, J], F32, name="neg_c")
+            nc.gpsimd.tensor_tensor(
+                out=neg_c[:, j0:j1], in0=lnp[key][:, j0:j1], in1=lnw[key][:, j0:j1], op=ALU.subtract
+            )
+            for j in range(j0, j1):
+                shifts[(g, j)] = neg_c[:, j : j + 1]
+
+        def ln_table(key):
+            g, j0, j1 = key
             y = small.tile([P, J], F32, name="y")
-            lne[g] = y
-            nc.scalar.activation(out=y[:], in_=esums[g][:], func=ACT.Ln)
+            lne[key] = y
+            nc.scalar.activation(out=y[:, j0:j1], in_=esums[g][:, j0:j1], func=ACT.Ln)
 
-        def ln_table_shift(g):
-            shifts[g] = small.tile([P, J], F32, name="neg_c")
-            nc.vector.tensor_tensor(out=shifts[g][:], in0=negs[g][:], in1=lne[g][:], op=ALU.subtract)
+        def ln_table_shift(key):
+            g, j0, j1 = key
+            neg_c = small.tile([P, J], F32, name="neg_c")
+            nc.vector.tensor_tensor(
+                out=neg_c[:, j0:j1], in0=negs[g][:, j0:j1], in1=lne[key][:, j0:j1], op=ALU.subtract
+            )
+            for j in range(j0, j1):
+                shifts[(g, j)] = neg_c[:, j : j + 1]
 
-        def subtract_store(v, engines):
+        def subtract_store(v, engines, between=()):
             g, h = divmod(v, 2)
             lt = lts[g]
             for jj in range(JH):
                 j = h * JH + jj
-                shift = shifts[g][:, j : j + 1]
+                shift = shifts[(g, j)]
                 engine = engines[jj]
                 if engine == "V":
                     nc.vector.tensor_scalar(
@@ -528,6 +582,8 @@ def tile_binarymlp_pb_t_kernel(tc, z2, g2, beta2, W3, b3, out):
                     nc.scalar.activation(
                         out=lt[:, j, :], in_=lt[:, j, :], func=ACT.Identity, bias=shift, scale=1.0
                     )
+                if jj < len(between):
+                    between[jj]()
             nc.sync.dma_start(
                 out=out[v * UB : (v + 1) * UB, :].rearrange("(p j) c -> p j c", j=JH),
                 in_=lt[:, h * JH : (h + 1) * JH, :],
@@ -537,24 +593,26 @@ def tile_binarymlp_pb_t_kernel(tc, z2, g2, beta2, W3, b3, out):
         for t in range(4):
             affine_v(0, t)
             if t < 2:
-                late_tile(0, t + 2)
                 late_words(1, t)
             else:
                 late_tile(1, t - 2)
         regroup(0, 0, 0, UB, "V")
-        regroup(0, 1, 0, UB, "V")
         affine_s(1)
-        late_words(2, 0)
-        late_words(2, 1)
+        late_tile(1, 2)
+        late_tile(1, 3)
+        regroup(0, 1, 0, UB, "V")
         regroup(1, 1, 0, UB, "G")
-        regroup(1, 0, 0, UB, "S")
         quant(0)
         keep_warm(N_KEEP)
         for jj in range(JH):
             mx(0, jj)
         for t in range(4):
             affine_v(1, t)
-            late_tile(1 if t < 2 else 2, (t + 2) % 4)
+            if t < 2:
+                late_words(2, t)
+            else:
+                late_tile(2, t - 2)
+        regroup(1, 0, 0, UB, "S")
         affine_s(2)
         late_words(3, 0)
         late_words(3, 1)
@@ -562,17 +620,24 @@ def tile_binarymlp_pb_t_kernel(tc, z2, g2, beta2, W3, b3, out):
         for v in range(U - 2):
             g_a, t_a = (v + 4) // 2, 2 * (v % 2)
             g_t, t_t = (v + 5) // 2, 2 * ((v + 1) % 2)
-            g_p = (v - 3) // 2 if v % 2 == 1 and v >= 3 else -1
-            g_l = (v - 4) // 2 if v % 2 == 0 and v >= 4 else -1
+            key_p = ((v - 3) // 2, 0, J)
+            key_l = ((v - 4) // 2, 0, J)
+            key_s = ((v - 5) // 2, 0, J)
+            odd = v % 2 == 1
+            if odd and v >= 5:
+                ln_mul(key_s)
+            regroup(v + 2, 0, 0, UB, "S")
+            regroup(v + 2, 1, 0, UB, "G")
+            if odd and v >= 5:
+                ln_shift(key_s)
+            if odd and v >= 3:
+                ln_pow(key_p)
+            if not odd and v >= 4:
+                ln_diff(key_l)
             if v + 3 < U:
                 affine_s(v + 3)
-            regroup(v + 2, 1, 0, UB, "G")
-            regroup(v + 2, 0, 0, UB, "S")
-            if g_p >= 0:
-                ln_pow(g_p)
-            if g_l >= 0:
-                ln_guess(g_l)
-                ln_exp(g_l)
+            if not odd and v >= 4:
+                ln_exp(key_l)
             for jj in range(JH):
                 add_bias(v, jj)
                 mx(v + 1, jj)
@@ -589,42 +654,60 @@ def tile_binarymlp_pb_t_kernel(tc, z2, g2, beta2, W3, b3, out):
                     late_words(v + 4, jj - 2)
                 if jj == 2:
                     quant(v + 2)
-            if g_p >= 0:
-                ln_recip(g_p)
+            if odd and v >= 3:
+                ln_recip(key_p)
             if v >= 1:
                 expsum(v - 1)
             if v >= 5:
-                subtract_store(v - 5, "GGVV")
-            if g_l >= 0:
-                ln_step(g_l)
-        ln_guess(G - 3)
-        ln_exp(G - 3)
-        ln_step(G - 3)
+                between = () if odd or v < 4 else (lambda: ln_first(key_l), lambda: ln_second(key_l))
+                subtract_store(v - 5, "GGGG", between)
+            elif v == 4:
+                ln_first(key_l)
+                ln_second(key_l)
+        key_a = (G - 3, 0, J)
+        key_b = (G - 2, 0, J)
+        key_c = (G - 1, 0, JH)
+        row_max(U - 3, JH - 1, JH)
+        ln_diff(key_a)
+        ln_exp(key_a)
+        expsum(U - 3)
+        ln_pow(key_b)
+        ln_first(key_a)
+        ln_mul(key_a)
         for jj in range(JH):
             add_bias(U - 2, jj)
             mx(U - 1, jj)
-            if jj == 0:
-                row_max(U - 3, JH - 1, JH)
-                expsum(U - 3)
-                ln_pow(G - 2)
-            else:
+            if jj > 0:
                 row_max(U - 2, jj - 1, jj)
         row_max(U - 2, JH - 1, JH)
-        ln_recip(G - 2)
-        subtract_store(U - 7, "SSSV")
-        ln_guess(G - 2)
-        ln_exp(G - 2)
-        ln_step(G - 2)
+        ln_recip(key_b)
+        ln_second(key_a)
+        subtract_store(U - 7, "SGGS", (lambda: None, lambda: ln_shift(key_a), lambda: ln_diff(key_b)))
+        ln_exp(key_b)
+        ln_first(key_b)
         expsum(U - 2)
+        ln_pow(key_c)
+        ln_second(key_b)
+        ln_mul(key_b)
         for jj in range(JH):
             add_bias(U - 1, jj)
-            row_max(U - 1, jj, jj + 1)
-        subtract_store(U - 6, "GGVV")
-        subtract_store(U - 5, "GGVV")
-        expsum(U - 1)
-        subtract_store(U - 4, "VVVV")
-        subtract_store(U - 3, "VVVV")
-        ln_table(G - 1)
-        ln_table_shift(G - 1)
-        subtract_store(U - 2, "VVVV")
-        subtract_store(U - 1, "SSVV")
+            if jj > 0:
+                row_max(U - 1, jj - 1, jj)
+        row_max(U - 1, JH - 1, JH)
+        subtract_store(U - 6, "SGGV", (lambda: None, lambda: ln_shift(key_b)))
+        ln_recip(key_c)
+        ln_diff(key_c)
+        expsum(U - 1, 0, 2)
+        subtract_store(U - 5, "VGGV", (lambda: None, lambda: ln_first(key_c)))
+        ln_exp(key_c)
+        expsum(U - 1, 2, JH)
+        ln_second(key_c)
+        last = (G - 1, JH, J)
+        ln_table(last)
+        ln_mul(key_c)
+        subtract_store(U - 4, "GVVV")
+        ln_shift(key_c)
+        subtract_store(U - 3, "VGGV")
+        subtract_store(U - 2, "VGVG")
+        ln_table_shift(last)
+        subtract_store(U - 1, "VSSV")

@@ -27,16 +27,11 @@ JH = UB // P
 J = GB // P
 BN_EPS = 1e-5
 ROOT = 1024.0
-N_WARM = 12
-G_PIECE = 512
+N_WARM = 5
 N_KEEP = 6
-G_W = 1
-G_WT = 3
+G_W = 5
 CHUNK = 256
 NCH = B // CHUNK
-S_GROUPS = tuple(range(1, G, 2))
-NS = len(S_GROUPS)
-NV = 2 * NCH - 2 * NS
 INV = 1.0 / CHUNK
 NG = 3
 
@@ -57,17 +52,26 @@ def tile_binarymlp_pb_t_kernel(tc, z2, g2, beta2, W3, b3, out):
         pst = ctx.enter_context(tc.psum_pool(name="pst", bufs=4))
         ctx.enter_context(tc.manual_schedule())
 
-        brow = const.tile([P, C], BF16, name="brow")
-        nc.vector.memset(brow[:], 0.0)
-        vecs = const.tile([P, PASS_K], BF16, name="vecs")
-        nc.vector.memset(vecs[:], 0.0)
-        nc.sync.dma_start(out=brow[0:1, :], in_=b3.rearrange("(o c) -> o c", o=1))
-        nc.sync.dma_start(out=vecs[0:2, :], in_=g2.rearrange("(c x) -> c x", x=PASS_K))
-        nc.sync.dma_start(out=vecs[2:4, :], in_=beta2.rearrange("(c x) -> c x", x=PASS_K))
+        zns = []
+        for g in range(G):
+            zn = big.tile([P, J, K], BF16, tag="big", name="zn%d" % g, align_bytes=64)
+            zns.append(zn)
+
+        def load(u):
+            g, h = divmod(u, 2)
+            rows_u = z2[u * UB : (u + 1) * UB, :].rearrange("(p j) k -> p j k", j=JH)
+            n = JH if u == 0 else 1
+            for i in range(n):
+                j0, j1 = i * JH // n, (i + 1) * JH // n
+                nc.sync.dma_start(out=zns[g][:, h * JH + j0 : h * JH + j1, :], in_=rows_u[:, j0:j1, :])
+
+        load(0)
+        load(1)
+
         wcodes = const.tile([P, 2 * C], U32, name="wcodes", align_bytes=64)
         wscl = const.tile([P, 2 * C], U8, name="wscl", align_bytes=64)
-        nc.vector.memset(wcodes[:, 0:C].bitcast(I32), 0)
         nc.vector.memset(wscl[:, 0:C].bitcast(I32), 0)
+        nc.vector.memset(wcodes[:, 0:C].bitcast(I32), 0)
         one = const.tile([P, 1], F32, name="one")
         nc.vector.memset(one[:], 1.0)
         warm = const.tile([P, 1], F32, name="warm")
@@ -85,6 +89,14 @@ def tile_binarymlp_pb_t_kernel(tc, z2, g2, beta2, W3, b3, out):
                 stop=True,
             )
 
+        brow = const.tile([P, C], BF16, name="brow")
+        nc.vector.memset(brow[:], 0.0)
+        vecs = const.tile([P, PASS_K], BF16, name="vecs")
+        nc.vector.memset(vecs[:], 0.0)
+        nc.sync.dma_start(out=brow[0:1, :], in_=b3.rearrange("(o c) -> o c", o=1))
+        nc.sync.dma_start(out=vecs[0:2, :], in_=g2.rearrange("(c x) -> c x", x=PASS_K))
+        nc.sync.dma_start(out=vecs[2:4, :], in_=beta2.rearrange("(c x) -> c x", x=PASS_K))
+
         ident = const.tile([P, P], BF16, name="ident")
         make_identity(nc, ident[:])
         identf = const.tile([P, P], F32, name="identf")
@@ -96,38 +108,27 @@ def tile_binarymlp_pb_t_kernel(tc, z2, g2, beta2, W3, b3, out):
         pe_pos = const.tile([P, J], F32, name="pe_pos")
         nc.gpsimd.memset(pe_pos[:], 1.0 / ROOT)
 
-        bs = const.tile([P, (NV + 1) * 6], F32, name="bs")
-        msq = const.tile([P, 2 * NV], F32, name="msq")
-        qsum = const.tile([P, 2, NV + NS], F32, name="qsum")
+        bs = const.tile([P, 2 * NCH * 6], F32, name="bs")
+        msq = const.tile([P, 4 * NCH], F32, name="msq")
+        qsum = const.tile([P, 2, 2 * NCH], F32, name="qsum")
         sq = const.tile([P, U], F32, name="sq")
         ab = const.tile([P, 4 * P], F32, name="ab", align_bytes=64)
         nc.gpsimd.memset(ab[:], 0.0)
         rows = const.tile([P, PASS_K], F32, name="rows", align_bytes=64)
         nc.gpsimd.memset(rows[:], 0.0)
         stat = const.tile([P, 2 * KT], F32, name="stat")
-        junk_s = const.tile([P, 3, UB], BF16, name="junk_s")
+        junk_s = const.tile([P, 2, UB], BF16, name="junk_s")
         junk_e = const.tile([P, JH, C], BF16, name="junk_e")
         junk_d = const.tile([P, NG, P], F32, name="junk_d")
         gb = const.tile([P, 2 * KT], F32, name="gb")
         bias_bc = const.tile([P, C], F32, name="bias_bc")
 
-        pv = pst.tile([P, 4, P], BF16, tag="tr", name="pv")
-        for t in range(4):
-            nc.tensor.transpose(pv[:, t, :], vecs[:, t:PASS_K:4], ident[:])
-        nc.vector.tensor_copy(
-            out=gb[:].rearrange("p (r t) -> p r t", t=4), in_=pv[:, :, 0:4].rearrange("p t r -> p r t")
-        )
-        pb = pst.tile([P, C], F32, tag="tr", name="pb")
-        nc.tensor.matmul(out=pb[:], lhsT=ones[:], rhs=brow[:], start=True, stop=True)
-        nc.scalar.copy(out=bias_bc[:], in_=pb[:])
-
         grams = []
         for i in range(NG):
             grams.append(psa.tile([P, P], F32, tag="acc", name="gram%d" % i))
-        psums = psa.tile([P, 4 * U + 2 * NS], F32, tag="acc", name="psums")
+        psums = psa.tile([P, 4 * U], F32, tag="acc", name="psums")
         plain = [(0, 0), (0, 1), (1, 0), (1, 1)]
         cols = [c * PASS_K + 256 + h * P for c, h in plain]
-        n_v = [0, NCH]
 
         gw = st.tile([P, 2, C, 4], BF16, tag="st", name="gw", align_bytes=64)
 
@@ -146,89 +147,76 @@ def tile_binarymlp_pb_t_kernel(tc, z2, g2, beta2, W3, b3, out):
                     in_=pw[:, i, :, :].rearrange("p u n -> p n u"),
                 )
 
-        zns = []
-        for g in range(G):
-            zn = big.tile([P, J, K], BF16, tag="big", name="zn%d" % g, align_bytes=64)
-            zns.append(zn)
-            for h in range(2):
-                u = 2 * g + h
-                nc.sync.dma_start(
-                    out=zn[:, h * JH : (h + 1) * JH, :],
-                    in_=z2[u * UB : (u + 1) * UB, :].rearrange("(p j) k -> p j k", j=JH),
+        def small_vectors():
+            pv = pst.tile([P, 4, P], BF16, tag="tr", name="pv")
+            for t in range(4):
+                nc.tensor.transpose(pv[:, t, :], vecs[:, t:PASS_K:4], ident[:])
+            nc.vector.tensor_copy(
+                out=gb[:].rearrange("p (r t) -> p r t", t=4), in_=pv[:, :, 0:4].rearrange("p t r -> p r t")
+            )
+            pb = pst.tile([P, C], F32, tag="tr", name="pb")
+            nc.tensor.matmul(out=pb[:], lhsT=ones[:], rhs=brow[:], start=True, stop=True)
+            nc.scalar.copy(out=bias_bc[:], in_=pb[:])
+
+        def words(u, c):
+            g, h = divmod(u, 2)
+            pw2 = pst.tile([P, UB], F32, tag="tr", name="pw2")
+            zw = zns[g][:].bitcast(F32)
+            for j in range(JH):
+                nc.tensor.transpose(
+                    pw2[:, j * P : (j + 1) * P], zw[:, h * JH + j, 256 * c : 256 * c + P], identf[:]
                 )
-            if g == G_W:
+            return pw2
+
+        def word_stats(u, c, pw2):
+            pairs = pw2[:].bitcast(BF16)
+            for q in range(2):
+                n = (c * NCH + 2 * u + q) * 6
+                nc.vector.bn_stats(out=bs[:, n : n + 6], in_=pairs[:, q * 512 : (q + 1) * 512])
+
+        ahead = words(0, 0)
+        for u in range(U):
+            g, h = divmod(u, 2)
+            if h == 1 and g + 1 < G:
+                load(u + 1)
+                load(u + 2)
+            if u == 2:
+                small_vectors()
+            if u == 2 * G_W:
                 wn = st.tile([P, C // P, K], BF16, tag="st", name="wn", align_bytes=64)
                 nc.sync.dma_start(out=wn[:], in_=W3.rearrange("(t p) k -> p t k", p=P))
-            zw = zn[:].bitcast(F32)
-            for h in range(2):
-                u = 2 * g + h
-                js = range(h * JH, (h + 1) * JH)
-                pws = []
-                for c in range(2):
-                    pw2 = pst.tile([P, JH * P], F32, tag="tr", name="pw2")
-                    pws.append(pw2[:].bitcast(BF16))
-                    for j in range(JH):
-                        nc.tensor.transpose(
-                            pw2[:, j * P : (j + 1) * P], zw[:, h * JH + j, 256 * c : 256 * c + P], identf[:]
-                        )
-                pt = pst.tile([P, UB], BF16, tag="tr", name="pt")
-                for j in range(JH):
-                    nc.tensor.transpose(
-                        pt[:, j * P : (j + 1) * P], zn[:, h * JH + j, cols[3] : cols[3] + P], ident[:]
-                    )
-                for i in range(NG):
-                    for j in js:
-                        nc.tensor.matmul(
-                            out=grams[i][:],
-                            lhsT=zn[:, j, cols[i] : cols[i] + P],
-                            rhs=zn[:, j, cols[i] : cols[i] + P],
-                            start=(g == 0 and j == 0),
-                            stop=(g == G - 1 and j == J - 1),
-                        )
-                for i in range(4):
-                    for j in js:
-                        nc.tensor.matmul(
-                            out=psums[:, i * U + u : i * U + u + 1],
-                            lhsT=zn[:, j, cols[i] : cols[i] + P],
-                            rhs=inv_col[:],
-                            start=(j == js[0]),
-                            stop=(j == js[-1]),
-                        )
-                on_scalar = h == 0 and g in S_GROUPS
-                if on_scalar:
-                    s_col = S_GROUPS.index(g)
-                    for e in range(2):
-                        for j in js:
-                            nc.tensor.matmul(
-                                out=psums[:, 4 * U + e * NS + s_col : 4 * U + e * NS + s_col + 1],
-                                lhsT=zn[:, j, PASS_K + e : PASS_K + 256 : 2],
-                                rhs=inv_col[:],
-                                start=(j == js[0]),
-                                stop=(j == js[-1]),
-                            )
-                for c in range(2):
-                    if c == 1 and on_scalar:
-                        for e in range(2):
-                            nc.scalar.activation(
-                                out=junk_s[:, e, :],
-                                in_=pws[c][:, e : 2 * UB : 2],
-                                func=ACT.Square,
-                                accum_out=qsum[:, e, NV + s_col : NV + s_col + 1],
-                            )
-                    else:
-                        for q in range(2):
-                            n = n_v[c] * 6
-                            n_v[c] += 1
-                            nc.vector.bn_stats(out=bs[:, n : n + 6], in_=pws[c][:, q * 512 : (q + 1) * 512])
-                nc.scalar.activation(out=junk_s[:, 2, :], in_=pt[:], func=ACT.Square, accum_out=sq[:, u : u + 1])
-            if g >= G_WT and g < G_WT + 4:
-                w_bank(g - G_WT)
-            if g == G_WT + 3:
-                nc.vector.quantize_mx(
-                    out=wcodes[:].bitcast(FP8X4),
-                    scales=wscl[:],
-                    in_=gw[:].rearrange("p c n t -> p (c n t)"),
+            zn = zns[g]
+            js = range(h * JH, (h + 1) * JH)
+            first = ahead
+            second = words(u, 1)
+            pt = pst.tile([P, UB], BF16, tag="tr", name="pt")
+            for j in range(JH):
+                nc.tensor.transpose(
+                    pt[:, j * P : (j + 1) * P], zn[:, h * JH + j, cols[3] : cols[3] + P], ident[:]
                 )
+            word_stats(u, 0, first)
+            if u + 1 < U:
+                ahead = words(u + 1, 0)
+            for i in range(NG):
+                for j in js:
+                    nc.tensor.matmul(
+                        out=grams[i][:],
+                        lhsT=zn[:, j, cols[i] : cols[i] + P],
+                        rhs=zn[:, j, cols[i] : cols[i] + P],
+                        start=(u == 0 and j == 0),
+                        stop=(u == U - 1 and j == J - 1),
+                    )
+            for i in range(4):
+                for j in js:
+                    nc.tensor.matmul(
+                        out=psums[:, i * U + u : i * U + u + 1],
+                        lhsT=zn[:, j, cols[i] : cols[i] + P],
+                        rhs=inv_col[:],
+                        start=(j == js[0]),
+                        stop=(j == js[-1]),
+                    )
+            word_stats(u, 1, second)
+            nc.scalar.activation(out=junk_s[:, h, :], in_=pt[:], func=ACT.Square, accum_out=sq[:, u : u + 1])
 
         dts = {}
         wts = {}
@@ -253,29 +241,26 @@ def tile_binarymlp_pb_t_kernel(tc, z2, g2, beta2, W3, b3, out):
                 )
 
         late_tile(0, 0)
-        late_tile(0, 1)
-        late_words(0, 0)
-        late_words(0, 1)
+        w_bank(0)
+        w_bank(1)
 
         abv = ab[:].rearrange("p (u h x) -> p u h x", u=2, h=2)
         bsv = bs[:].rearrange("p (n e f) -> p e n f", e=2, f=3)
-        mean_v = bsv[:, :, 0:NV, 1]
-        nc.vector.tensor_reduce(
-            out=bsv[:, :, NV, 1],
-            in_=psums[:, 4 * U : 4 * U + 2 * NS].rearrange("p (e g) -> p e g", e=2),
-            axis=AX.X,
-            op=ALU.add,
-        )
+        mean_v = bsv[:, :, :, 1]
         nc.vector.tensor_tensor(
             out=msq[:].rearrange("p (e n) -> p e n", e=2), in0=mean_v, in1=mean_v, op=ALU.mult
         )
-        for c, n0, n1 in ((0, 0, NCH), (1, NCH, NV + 1)):
-            nc.vector.tensor_reduce(out=abv[:, 0, :, c], in_=bsv[:, :, n0:n1, 1], axis=AX.X, op=ALU.add)
+        nc.vector.tensor_reduce(
+            out=abv[:, 0, :, 0:2],
+            in_=bs[:].rearrange("p (c n e f) -> p e c n f", c=2, e=2, f=3)[:, :, :, :, 1],
+            axis=AX.X,
+            op=ALU.add,
+        )
         nc.vector.scalar_tensor_tensor(
-            out=qsum[:, :, 0:NV],
+            out=qsum[:],
             in0=msq[:].rearrange("p (e n) -> p e n", e=2),
             scalar=float(CHUNK),
-            in1=bsv[:, :, 0:NV, 2],
+            in1=bsv[:, :, :, 2],
             op0=ALU.mult,
             op1=ALU.add,
         )
@@ -290,11 +275,12 @@ def tile_binarymlp_pb_t_kernel(tc, z2, g2, beta2, W3, b3, out):
                 op1=ALU.mult,
                 accum_out=abv[:, 1, h, 2 + c : 3 + c],
             )
-        for c, n0, n1 in ((0, 0, NCH), (1, NCH, NV + NS)):
-            nc.vector.tensor_reduce(out=abv[:, 0, :, 2 + c], in_=qsum[:, :, n0:n1], axis=AX.X, op=ALU.add)
+        nc.vector.tensor_reduce(
+            out=abv[:, 0, :, 2:4], in_=qsum[:].rearrange("p e (c n) -> p e c n", c=2), axis=AX.X, op=ALU.add
+        )
         nc.vector.tensor_reduce(
             out=abv[:, 1, :, 0:2],
-            in_=psums[:, 0 : 4 * U].rearrange("p (c h u) -> p h c u", c=2, h=2),
+            in_=psums[:].rearrange("p (c h u) -> p h c u", c=2, h=2),
             axis=AX.X,
             op=ALU.add,
         )
@@ -302,6 +288,7 @@ def tile_binarymlp_pb_t_kernel(tc, z2, g2, beta2, W3, b3, out):
         pt1 = psa.tile([P, 4 * P], F32, tag="acc", name="pt1")
         for q in range(4):
             nc.tensor.transpose(pt1[:, q * P : (q + 1) * P], ab[:, q * P : (q + 1) * P], identf[:])
+        w_bank(2)
         rows_v = rows[0:4, :].rearrange("r (t p) -> r t p", t=4)
         for e in range(2):
             nc.vector.tensor_copy(
@@ -317,6 +304,10 @@ def tile_binarymlp_pb_t_kernel(tc, z2, g2, beta2, W3, b3, out):
         nc.vector.tensor_copy(
             out=stat[:].rearrange("p (r t) -> p r t", t=4), in_=pt2[:, :, 0:4].rearrange("p t r -> p r t")
         )
+        w_bank(3)
+        late_words(0, 0)
+        late_tile(0, 1)
+        late_words(0, 1)
         late_tile(0, 2, early=True)
         late_tile(0, 3, early=True)
         ssum = stat[:, 0:KT]
@@ -403,15 +394,14 @@ def tile_binarymlp_pb_t_kernel(tc, z2, g2, beta2, W3, b3, out):
             if engine == "V":
                 nc.vector.tensor_scalar(out=dst, in0=src, scalar1=0.0, scalar2=None, op0=ALU.max)
             elif engine == "G":
-                for n in range(b0, b1, G_PIECE):
-                    nc.gpsimd.tensor_scalar(
-                        out=ghs[v][:, c, n : n + G_PIECE, :],
-                        in0=four[:, :, n : n + G_PIECE].rearrange("p t n -> p n t"),
-                        scalar1=1.0,
-                        scalar2=0.0,
-                        op0=ALU.mult,
-                        op1=ALU.add,
-                    )
+                nc.gpsimd.tensor_scalar(
+                    out=ghs[v][:, c, b0:b1, :],
+                    in0=four[:, :, b0:b1].rearrange("p t n -> p n t"),
+                    scalar1=1.0,
+                    scalar2=0.0,
+                    op0=ALU.mult,
+                    op1=ALU.add,
+                )
             else:
                 nc.scalar.activation(out=dst, in_=src, func=ACT.Relu)
 
@@ -596,13 +586,21 @@ def tile_binarymlp_pb_t_kernel(tc, z2, g2, beta2, W3, b3, out):
                 late_words(1, t)
             else:
                 late_tile(1, t - 2)
+            if t == 1:
+                nc.vector.quantize_mx(
+                    out=wcodes[:].bitcast(FP8X4),
+                    scales=wscl[:],
+                    in_=gw[:].rearrange("p c n t -> p (c n t)"),
+                )
         regroup(0, 0, 0, UB, "V")
         affine_s(1)
         late_tile(1, 2)
         late_tile(1, 3)
-        regroup(0, 1, 0, UB, "V")
-        regroup(1, 1, 0, UB, "G")
+        for n in range(0, UB, P):
+            regroup(0, 1, n, n + P, "G")
         quant(0)
+        for n in range(0, UB, P):
+            regroup(1, 1, n, n + P, "G")
         keep_warm(N_KEEP)
         for jj in range(JH):
             mx(0, jj)
@@ -660,7 +658,7 @@ def tile_binarymlp_pb_t_kernel(tc, z2, g2, beta2, W3, b3, out):
                 expsum(v - 1)
             if v >= 5:
                 between = () if odd or v < 4 else (lambda: ln_first(key_l), lambda: ln_second(key_l))
-                subtract_store(v - 5, "GGGG", between)
+                subtract_store(v - 5, "GVGV", between)
             elif v == 4:
                 ln_first(key_l)
                 ln_second(key_l)
@@ -670,10 +668,12 @@ def tile_binarymlp_pb_t_kernel(tc, z2, g2, beta2, W3, b3, out):
         row_max(U - 3, JH - 1, JH)
         ln_diff(key_a)
         ln_exp(key_a)
+        ln_first(key_a)
+        ln_second(key_a)
+        ln_mul(key_a)
+        ln_shift(key_a)
         expsum(U - 3)
         ln_pow(key_b)
-        ln_first(key_a)
-        ln_mul(key_a)
         for jj in range(JH):
             add_bias(U - 2, jj)
             mx(U - 1, jj)
@@ -681,33 +681,35 @@ def tile_binarymlp_pb_t_kernel(tc, z2, g2, beta2, W3, b3, out):
                 row_max(U - 2, jj - 1, jj)
         row_max(U - 2, JH - 1, JH)
         ln_recip(key_b)
-        ln_second(key_a)
-        subtract_store(U - 7, "SGGS", (lambda: None, lambda: ln_shift(key_a), lambda: ln_diff(key_b)))
+        subtract_store(U - 7, "SGGS")
+        ln_diff(key_b)
         ln_exp(key_b)
         ln_first(key_b)
-        expsum(U - 2)
-        ln_pow(key_c)
         ln_second(key_b)
         ln_mul(key_b)
+        ln_shift(key_b)
+        expsum(U - 2)
+        subtract_store(U - 6, "GGGG")
+        ln_pow(key_c)
         for jj in range(JH):
             add_bias(U - 1, jj)
             if jj > 0:
                 row_max(U - 1, jj - 1, jj)
         row_max(U - 1, JH - 1, JH)
-        subtract_store(U - 6, "SGGV", (lambda: None, lambda: ln_shift(key_b)))
         ln_recip(key_c)
         ln_diff(key_c)
-        expsum(U - 1, 0, 2)
-        subtract_store(U - 5, "VGGV", (lambda: None, lambda: ln_first(key_c)))
+        subtract_store(U - 5, "VGGV")
+        expsum(U - 1, 0, 3)
         ln_exp(key_c)
-        expsum(U - 1, 2, JH)
+        expsum(U - 1, 3, JH)
+        ln_first(key_c)
         ln_second(key_c)
+        ln_mul(key_c)
+        ln_shift(key_c)
         last = (G - 1, JH, J)
         ln_table(last)
-        ln_mul(key_c)
-        subtract_store(U - 4, "GVVV")
-        ln_shift(key_c)
-        subtract_store(U - 3, "VGGV")
-        subtract_store(U - 2, "VGVG")
+        subtract_store(U - 4, "VGGV")
+        subtract_store(U - 3, "VVVV")
+        subtract_store(U - 2, "VGVV")
         ln_table_shift(last)
         subtract_store(U - 1, "VSSV")

@@ -72,6 +72,13 @@ def tile_binarymlp_pb_t_kernel(tc, z2, g2, beta2, W3, b3, out):
         wscl = const.tile([P, 2 * C], U8, name="wscl", align_bytes=64)
         nc.vector.memset(wscl[:, 0:C].bitcast(I32), 0)
         nc.vector.memset(wcodes[:, 0:C].bitcast(I32), 0)
+        brow = const.tile([P, C], BF16, name="brow")
+        nc.vector.memset(brow[:], 0.0)
+        vecs = const.tile([P, PASS_K], BF16, name="vecs")
+        nc.vector.memset(vecs[:], 0.0)
+        nc.scalar.dma_start(out=brow[0:1, :], in_=b3.rearrange("(o c) -> o c", o=1))
+        nc.scalar.dma_start(out=vecs[0:2, :], in_=g2.rearrange("(c x) -> c x", x=PASS_K))
+        nc.scalar.dma_start(out=vecs[2:4, :], in_=beta2.rearrange("(c x) -> c x", x=PASS_K))
         one = const.tile([P, 1], F32, name="one")
         nc.vector.memset(one[:], 1.0)
         warm = const.tile([P, 1], F32, name="warm")
@@ -89,14 +96,6 @@ def tile_binarymlp_pb_t_kernel(tc, z2, g2, beta2, W3, b3, out):
                 stop=True,
             )
 
-        brow = const.tile([P, C], BF16, name="brow")
-        nc.vector.memset(brow[:], 0.0)
-        vecs = const.tile([P, PASS_K], BF16, name="vecs")
-        nc.vector.memset(vecs[:], 0.0)
-        nc.sync.dma_start(out=brow[0:1, :], in_=b3.rearrange("(o c) -> o c", o=1))
-        nc.sync.dma_start(out=vecs[0:2, :], in_=g2.rearrange("(c x) -> c x", x=PASS_K))
-        nc.sync.dma_start(out=vecs[2:4, :], in_=beta2.rearrange("(c x) -> c x", x=PASS_K))
-
         ident = const.tile([P, P], BF16, name="ident")
         make_identity(nc, ident[:])
         identf = const.tile([P, P], F32, name="identf")
@@ -111,13 +110,13 @@ def tile_binarymlp_pb_t_kernel(tc, z2, g2, beta2, W3, b3, out):
         bs = const.tile([P, 2 * NCH * 6], F32, name="bs")
         msq = const.tile([P, 4 * NCH], F32, name="msq")
         qsum = const.tile([P, 2, 2 * NCH], F32, name="qsum")
-        sq = const.tile([P, U], F32, name="sq")
+        sq = const.tile([P, 2, U], F32, name="sq")
         ab = const.tile([P, 4 * P], F32, name="ab", align_bytes=64)
         nc.gpsimd.memset(ab[:], 0.0)
         rows = const.tile([P, PASS_K], F32, name="rows", align_bytes=64)
         nc.gpsimd.memset(rows[:], 0.0)
         stat = const.tile([P, 2 * KT], F32, name="stat")
-        junk_s = const.tile([P, 2, UB], BF16, name="junk_s")
+        junk_s = const.tile([P, 2, 2, UB], BF16, name="junk_s")
         junk_e = const.tile([P, JH, C], BF16, name="junk_e")
         junk_d = const.tile([P, NG, P], F32, name="junk_d")
         gb = const.tile([P, 2 * KT], F32, name="gb")
@@ -126,7 +125,7 @@ def tile_binarymlp_pb_t_kernel(tc, z2, g2, beta2, W3, b3, out):
         grams = []
         for i in range(NG):
             grams.append(psa.tile([P, P], F32, tag="acc", name="gram%d" % i))
-        psums = psa.tile([P, 4 * U], F32, tag="acc", name="psums")
+        psums = psa.tile([P, NG * U], F32, tag="acc", name="psums")
         plain = [(0, 0), (0, 1), (1, 0), (1, 1)]
         cols = [c * PASS_K + 256 + h * P for c, h in plain]
 
@@ -180,8 +179,6 @@ def tile_binarymlp_pb_t_kernel(tc, z2, g2, beta2, W3, b3, out):
             if h == 1 and g + 1 < G:
                 load(u + 1)
                 load(u + 2)
-            if u == 2:
-                small_vectors()
             if u == 2 * G_W:
                 wn = st.tile([P, C // P, K], BF16, tag="st", name="wn", align_bytes=64)
                 nc.sync.dma_start(out=wn[:], in_=W3.rearrange("(t p) k -> p t k", p=P))
@@ -206,7 +203,7 @@ def tile_binarymlp_pb_t_kernel(tc, z2, g2, beta2, W3, b3, out):
                         start=(u == 0 and j == 0),
                         stop=(u == U - 1 and j == J - 1),
                     )
-            for i in range(4):
+            for i in range(NG):
                 for j in js:
                     nc.tensor.matmul(
                         out=psums[:, i * U + u : i * U + u + 1],
@@ -216,7 +213,10 @@ def tile_binarymlp_pb_t_kernel(tc, z2, g2, beta2, W3, b3, out):
                         stop=(j == js[-1]),
                     )
             word_stats(u, 1, second)
-            nc.scalar.activation(out=junk_s[:, h, :], in_=pt[:], func=ACT.Square, accum_out=sq[:, u : u + 1])
+            nc.scalar.activation(out=junk_s[:, h, 0, :], in_=pt[:], func=ACT.Square, accum_out=sq[:, 1, u : u + 1])
+            nc.scalar.activation(
+                out=junk_s[:, h, 1, :], in_=pt[:], func=ACT.Copy, scale=INV, accum_out=sq[:, 0, u : u + 1]
+            )
 
         dts = {}
         wts = {}
@@ -240,7 +240,7 @@ def tile_binarymlp_pb_t_kernel(tc, z2, g2, beta2, W3, b3, out):
                     wt[:, j * P : (j + 1) * P], zw[:, h * JH + j, 256 + u : 512 : 2], identf[:]
                 )
 
-        late_tile(0, 0)
+        small_vectors()
         w_bank(0)
         w_bank(1)
 
@@ -279,15 +279,19 @@ def tile_binarymlp_pb_t_kernel(tc, z2, g2, beta2, W3, b3, out):
             out=abv[:, 0, :, 2:4], in_=qsum[:].rearrange("p e (c n) -> p e c n", c=2), axis=AX.X, op=ALU.add
         )
         nc.vector.tensor_reduce(
-            out=abv[:, 1, :, 0:2],
-            in_=psums[:].rearrange("p (c h u) -> p h c u", c=2, h=2),
+            out=abv[:, 1, :, 0],
+            in_=psums[:, 0 : 2 * U].rearrange("p (h u) -> p h u", h=2),
             axis=AX.X,
             op=ALU.add,
         )
-        nc.vector.tensor_reduce(out=abv[:, 1, 1, 3:4], in_=sq[:], axis=AX.X, op=ALU.add)
+        nc.vector.tensor_reduce(
+            out=abv[:, 1, 0, 1:2], in_=psums[:, 2 * U : 3 * U], axis=AX.X, op=ALU.add
+        )
+        nc.vector.tensor_reduce(out=abv[:, 1, 1, 1:4:2], in_=sq[:], axis=AX.X, op=ALU.add)
         pt1 = psa.tile([P, 4 * P], F32, tag="acc", name="pt1")
         for q in range(4):
             nc.tensor.transpose(pt1[:, q * P : (q + 1) * P], ab[:, q * P : (q + 1) * P], identf[:])
+        late_tile(0, 0)
         w_bank(2)
         rows_v = rows[0:4, :].rearrange("r (t p) -> r t p", t=4)
         for e in range(2):
@@ -553,7 +557,7 @@ def tile_binarymlp_pb_t_kernel(tc, z2, g2, beta2, W3, b3, out):
             for j in range(j0, j1):
                 shifts[(g, j)] = neg_c[:, j : j + 1]
 
-        def subtract_store(v, engines, between=()):
+        def subtract(v, engines, between=()):
             g, h = divmod(v, 2)
             lt = lts[g]
             for jj in range(JH):
@@ -568,16 +572,23 @@ def tile_binarymlp_pb_t_kernel(tc, z2, g2, beta2, W3, b3, out):
                     nc.gpsimd.tensor_scalar(
                         out=lt[:, j, :], in0=lt[:, j, :], scalar1=1.0, scalar2=shift, op0=ALU.mult, op1=ALU.add
                     )
-                else:
+                elif engine == "S":
                     nc.scalar.activation(
                         out=lt[:, j, :], in_=lt[:, j, :], func=ACT.Identity, bias=shift, scale=1.0
                     )
                 if jj < len(between):
                     between[jj]()
+
+        def store(v):
+            g, h = divmod(v, 2)
             nc.sync.dma_start(
                 out=out[v * UB : (v + 1) * UB, :].rearrange("(p j) c -> p j c", j=JH),
-                in_=lt[:, h * JH : (h + 1) * JH, :],
+                in_=lts[g][:, h * JH : (h + 1) * JH, :],
             )
+
+        def subtract_store(v, engines):
+            subtract(v, engines)
+            store(v)
 
         affine_s(0)
         for t in range(4):
@@ -596,20 +607,22 @@ def tile_binarymlp_pb_t_kernel(tc, z2, g2, beta2, W3, b3, out):
         affine_s(1)
         late_tile(1, 2)
         late_tile(1, 3)
-        for n in range(0, UB, P):
+        for n in range(0, UB - P, P):
             regroup(0, 1, n, n + P, "G")
+        for t in range(2):
+            affine_v(1, t)
+            late_words(2, t)
+        regroup(0, 1, UB - P, UB, "V")
         quant(0)
-        for n in range(0, UB, P):
+        for n in range(0, UB // 2, P):
             regroup(1, 1, n, n + P, "G")
         keep_warm(N_KEEP)
         for jj in range(JH):
             mx(0, jj)
-        for t in range(4):
+        for t in range(2, 4):
             affine_v(1, t)
-            if t < 2:
-                late_words(2, t)
-            else:
-                late_tile(2, t - 2)
+            late_tile(2, t - 2)
+        regroup(1, 1, UB // 2, UB, "V")
         regroup(1, 0, 0, UB, "S")
         affine_s(2)
         late_words(3, 0)
@@ -652,13 +665,18 @@ def tile_binarymlp_pb_t_kernel(tc, z2, g2, beta2, W3, b3, out):
                     late_words(v + 4, jj - 2)
                 if jj == 2:
                     quant(v + 2)
+                    if v >= 5:
+                        subtract(v - 5, "-V-V")
             if odd and v >= 3:
                 ln_recip(key_p)
             if v >= 1:
                 expsum(v - 1)
             if v >= 5:
-                between = () if odd or v < 4 else (lambda: ln_first(key_l), lambda: ln_second(key_l))
-                subtract_store(v - 5, "GVGV", between)
+                between = () if odd or v < 4 else (lambda: ln_first(key_l), lambda: None, lambda: ln_second(key_l))
+                subtract(v - 5, "G-G-", between)
+                store(v - 5)
+            if v == U - 3:
+                subtract_store(v - 4, "SSSS")
             elif v == 4:
                 ln_first(key_l)
                 ln_second(key_l)
@@ -673,7 +691,11 @@ def tile_binarymlp_pb_t_kernel(tc, z2, g2, beta2, W3, b3, out):
         ln_mul(key_a)
         ln_shift(key_a)
         expsum(U - 3)
+        subtract(U - 6, "GG--")
         ln_pow(key_b)
+        subtract(U - 6, "--GG")
+        store(U - 6)
+        subtract_store(U - 5, "SSSS")
         for jj in range(JH):
             add_bias(U - 2, jj)
             mx(U - 1, jj)
@@ -681,7 +703,6 @@ def tile_binarymlp_pb_t_kernel(tc, z2, g2, beta2, W3, b3, out):
                 row_max(U - 2, jj - 1, jj)
         row_max(U - 2, JH - 1, JH)
         ln_recip(key_b)
-        subtract_store(U - 7, "SGGS")
         ln_diff(key_b)
         ln_exp(key_b)
         ln_first(key_b)
@@ -689,7 +710,7 @@ def tile_binarymlp_pb_t_kernel(tc, z2, g2, beta2, W3, b3, out):
         ln_mul(key_b)
         ln_shift(key_b)
         expsum(U - 2)
-        subtract_store(U - 6, "GGGG")
+        subtract(U - 4, "GG--")
         ln_pow(key_c)
         for jj in range(JH):
             add_bias(U - 1, jj)
@@ -697,19 +718,19 @@ def tile_binarymlp_pb_t_kernel(tc, z2, g2, beta2, W3, b3, out):
                 row_max(U - 1, jj - 1, jj)
         row_max(U - 1, JH - 1, JH)
         ln_recip(key_c)
+        subtract(U - 4, "--GV")
+        store(U - 4)
         ln_diff(key_c)
-        subtract_store(U - 5, "VGGV")
         expsum(U - 1, 0, 3)
         ln_exp(key_c)
         expsum(U - 1, 3, JH)
         ln_first(key_c)
         ln_second(key_c)
+        subtract_store(U - 3, "VGVV")
         ln_mul(key_c)
         ln_shift(key_c)
         last = (G - 1, JH, J)
         ln_table(last)
-        subtract_store(U - 4, "VGGV")
-        subtract_store(U - 3, "VVVV")
         subtract_store(U - 2, "VGVV")
         ln_table_shift(last)
         subtract_store(U - 1, "VSSV")

@@ -28,6 +28,8 @@ J = GB // P
 BN_EPS = 1e-5
 ROOT = 1024.0
 N_WARM = 5
+N_HEAT = 4
+HEAT = 256
 N_KEEP = 6
 G_W = 5
 CHUNK = 256
@@ -125,7 +127,7 @@ def tile_binarymlp_pb_t_kernel(tc, z2, g2, beta2, W3, b3, out):
         grams = []
         for i in range(NG):
             grams.append(psa.tile([P, P], F32, tag="acc", name="gram%d" % i))
-        psums = psa.tile([P, NG * U], F32, tag="acc", name="psums")
+        psums = psa.tile([P, C], F32, tag="acc", name="psums")
         plain = [(0, 0), (0, 1), (1, 0), (1, 1)]
         cols = [c * PASS_K + 256 + h * P for c, h in plain]
 
@@ -150,12 +152,10 @@ def tile_binarymlp_pb_t_kernel(tc, z2, g2, beta2, W3, b3, out):
             pv = pst.tile([P, 4, P], BF16, tag="tr", name="pv")
             for t in range(4):
                 nc.tensor.transpose(pv[:, t, :], vecs[:, t:PASS_K:4], ident[:])
-            nc.vector.tensor_copy(
-                out=gb[:].rearrange("p (r t) -> p r t", t=4), in_=pv[:, :, 0:4].rearrange("p t r -> p r t")
-            )
             pb = pst.tile([P, C], F32, tag="tr", name="pb")
             nc.tensor.matmul(out=pb[:], lhsT=ones[:], rhs=brow[:], start=True, stop=True)
             nc.scalar.copy(out=bias_bc[:], in_=pb[:])
+            return pv
 
         def words(u, c):
             g, h = divmod(u, 2)
@@ -194,6 +194,17 @@ def tile_binarymlp_pb_t_kernel(tc, z2, g2, beta2, W3, b3, out):
             word_stats(u, 0, first)
             if u + 1 < U:
                 ahead = words(u + 1, 0)
+            if u == 0:
+                for i in range(N_HEAT):
+                    nc.tensor.matmul_mx(
+                        out=psums[:, C - HEAT : C],
+                        lhsT=wcodes[:, 0:P].bitcast(FP8X4),
+                        lhsT_scale=wscl[:, 0:P],
+                        rhs=wcodes[:, 0:HEAT].bitcast(FP8X4),
+                        rhs_scale=wscl[:, 0:HEAT],
+                        start=True,
+                        stop=True,
+                    )
             for i in range(NG):
                 for j in js:
                     nc.tensor.matmul(
@@ -240,7 +251,7 @@ def tile_binarymlp_pb_t_kernel(tc, z2, g2, beta2, W3, b3, out):
                     wt[:, j * P : (j + 1) * P], zw[:, h * JH + j, 256 + u : 512 : 2], identf[:]
                 )
 
-        small_vectors()
+        pv = small_vectors()
         w_bank(0)
         w_bank(1)
 
@@ -288,10 +299,12 @@ def tile_binarymlp_pb_t_kernel(tc, z2, g2, beta2, W3, b3, out):
             out=abv[:, 1, 0, 1:2], in_=psums[:, 2 * U : 3 * U], axis=AX.X, op=ALU.add
         )
         nc.vector.tensor_reduce(out=abv[:, 1, 1, 1:4:2], in_=sq[:], axis=AX.X, op=ALU.add)
+        nc.vector.tensor_copy(
+            out=gb[:].rearrange("p (r t) -> p r t", t=4), in_=pv[:, :, 0:4].rearrange("p t r -> p r t")
+        )
         pt1 = psa.tile([P, 4 * P], F32, tag="acc", name="pt1")
         for q in range(4):
             nc.tensor.transpose(pt1[:, q * P : (q + 1) * P], ab[:, q * P : (q + 1) * P], identf[:])
-        late_tile(0, 0)
         w_bank(2)
         rows_v = rows[0:4, :].rearrange("r (t p) -> r t p", t=4)
         for e in range(2):
@@ -308,6 +321,7 @@ def tile_binarymlp_pb_t_kernel(tc, z2, g2, beta2, W3, b3, out):
         nc.vector.tensor_copy(
             out=stat[:].rearrange("p (r t) -> p r t", t=4), in_=pt2[:, :, 0:4].rearrange("p t r -> p r t")
         )
+        late_tile(0, 0)
         w_bank(3)
         late_words(0, 0)
         late_tile(0, 1)

@@ -28,10 +28,11 @@ J = GB // P
 BN_EPS = 1e-5
 ROOT = 1024.0
 N_WARM = 5
-N_HEAT = 4
+WEAVE = 2
 HEAT = 256
+HEAT_U = 2
 N_KEEP = 6
-G_W = 5
+G_W = 7
 CHUNK = 256
 NCH = B // CHUNK
 INV = 1.0 / CHUNK
@@ -157,15 +158,9 @@ def tile_binarymlp_pb_t_kernel(tc, z2, g2, beta2, W3, b3, out):
             nc.scalar.copy(out=bias_bc[:], in_=pb[:])
             return pv
 
-        def words(u, c):
+        def word_tile(u, c, j):
             g, h = divmod(u, 2)
-            pw2 = pst.tile([P, UB], F32, tag="tr", name="pw2")
-            zw = zns[g][:].bitcast(F32)
-            for j in range(JH):
-                nc.tensor.transpose(
-                    pw2[:, j * P : (j + 1) * P], zw[:, h * JH + j, 256 * c : 256 * c + P], identf[:]
-                )
-            return pw2
+            return zns[g][:].bitcast(F32)[:, h * JH + j, 256 * c : 256 * c + P]
 
         def word_stats(u, c, pw2):
             pairs = pw2[:].bitcast(BF16)
@@ -173,7 +168,22 @@ def tile_binarymlp_pb_t_kernel(tc, z2, g2, beta2, W3, b3, out):
                 n = (c * NCH + 2 * u + q) * 6
                 nc.vector.bn_stats(out=bs[:, n : n + 6], in_=pairs[:, q * 512 : (q + 1) * 512])
 
-        ahead = words(0, 0)
+        def heat(n):
+            for i in range(n):
+                nc.tensor.matmul_mx(
+                    out=psums[:, C - HEAT : C],
+                    lhsT=wcodes[:, 0:P].bitcast(FP8X4),
+                    lhsT_scale=wscl[:, 0:P],
+                    rhs=wcodes[:, 0:HEAT].bitcast(FP8X4),
+                    rhs_scale=wscl[:, 0:HEAT],
+                    start=True,
+                    stop=True,
+                )
+
+        ahead = pst.tile([P, UB], F32, tag="tr", name="pw2")
+        for j in range(JH):
+            nc.tensor.transpose(ahead[:, j * P : (j + 1) * P], word_tile(0, 0, j), identf[:])
+            heat(1)
         for u in range(U):
             g, h = divmod(u, 2)
             if h == 1 and g + 1 < G:
@@ -184,29 +194,11 @@ def tile_binarymlp_pb_t_kernel(tc, z2, g2, beta2, W3, b3, out):
                 nc.sync.dma_start(out=wn[:], in_=W3.rearrange("(t p) k -> p t k", p=P))
             zn = zns[g]
             js = range(h * JH, (h + 1) * JH)
-            first = ahead
-            second = words(u, 1)
-            pt = pst.tile([P, UB], BF16, tag="tr", name="pt")
-            for j in range(JH):
-                nc.tensor.transpose(
-                    pt[:, j * P : (j + 1) * P], zn[:, h * JH + j, cols[3] : cols[3] + P], ident[:]
-                )
-            word_stats(u, 0, first)
-            if u + 1 < U:
-                ahead = words(u + 1, 0)
-            if u == 0:
-                for i in range(N_HEAT):
-                    nc.tensor.matmul_mx(
-                        out=psums[:, C - HEAT : C],
-                        lhsT=wcodes[:, 0:P].bitcast(FP8X4),
-                        lhsT_scale=wscl[:, 0:P],
-                        rhs=wcodes[:, 0:HEAT].bitcast(FP8X4),
-                        rhs_scale=wscl[:, 0:HEAT],
-                        start=True,
-                        stop=True,
-                    )
-            for i in range(NG):
-                for j in js:
+            squares = [(i, j) for i in range(NG) for j in js]
+            sums = [(i, j) for i in range(NG) for j in js]
+
+            def weave(n):
+                for i, j in squares[n * WEAVE : (n + 1) * WEAVE]:
                     nc.tensor.matmul(
                         out=grams[i][:],
                         lhsT=zn[:, j, cols[i] : cols[i] + P],
@@ -214,8 +206,7 @@ def tile_binarymlp_pb_t_kernel(tc, z2, g2, beta2, W3, b3, out):
                         start=(u == 0 and j == 0),
                         stop=(u == U - 1 and j == J - 1),
                     )
-            for i in range(NG):
-                for j in js:
+                for i, j in sums[n * WEAVE : (n + 1) * WEAVE]:
                     nc.tensor.matmul(
                         out=psums[:, i * U + u : i * U + u + 1],
                         lhsT=zn[:, j, cols[i] : cols[i] + P],
@@ -223,6 +214,28 @@ def tile_binarymlp_pb_t_kernel(tc, z2, g2, beta2, W3, b3, out):
                         start=(j == js[0]),
                         stop=(j == js[-1]),
                     )
+
+            first = ahead
+            second = pst.tile([P, UB], F32, tag="tr", name="pw2")
+            pt = pst.tile([P, UB], BF16, tag="tr", name="pt")
+            if u + 1 < U:
+                ahead = pst.tile([P, UB], F32, tag="tr", name="pw2")
+            n_t = 0
+            for kind in range(3):
+                for j in range(JH):
+                    cut = slice(j * P, (j + 1) * P)
+                    if kind == 0:
+                        nc.tensor.transpose(second[:, cut], word_tile(u, 1, j), identf[:])
+                    elif kind == 1:
+                        nc.tensor.transpose(pt[:, cut], zn[:, h * JH + j, cols[3] : cols[3] + P], ident[:])
+                    elif u + 1 < U:
+                        nc.tensor.transpose(ahead[:, cut], word_tile(u + 1, 0, j), identf[:])
+                    n_t += 1
+                    if n_t % WEAVE == 0:
+                        weave(n_t // WEAVE - 1)
+                        if u < HEAT_U and n_t % JH == 0:
+                            heat(2)
+            word_stats(u, 0, first)
             word_stats(u, 1, second)
             nc.scalar.activation(out=junk_s[:, h, 0, :], in_=pt[:], func=ACT.Square, accum_out=sq[:, 1, u : u + 1])
             nc.scalar.activation(
@@ -740,11 +753,11 @@ def tile_binarymlp_pb_t_kernel(tc, z2, g2, beta2, W3, b3, out):
         expsum(U - 1, 3, JH)
         ln_first(key_c)
         ln_second(key_c)
-        subtract_store(U - 3, "VGVV")
         ln_mul(key_c)
         ln_shift(key_c)
         last = (G - 1, JH, J)
         ln_table(last)
-        subtract_store(U - 2, "VGVV")
+        subtract_store(U - 3, "VVVV")
+        subtract_store(U - 2, "GVVG")
         ln_table_shift(last)
         subtract_store(U - 1, "VSSV")

from contextlib import ExitStack

import concourse.mybir as mybir
from concourse.masks import make_identity

F32 = mybir.dt.float32
BF16 = mybir.dt.bfloat16
U32 = mybir.dt.uint32
U8 = mybir.dt.uint8
I32 = mybir.dt.int32
FP8X4 = mybir.dt.float8_e4m3fn_x4
ALU = mybir.AluOpType
ACT = mybir.ActivationFunctionType
AX = mybir.AxisListType

P = 128
B = 8192
K = 1024
C = 512
KT = K // P
PASS_K = 4 * P
G = 8
GB = B // G
U = 16
UB = B // U
JH = UB // P
J = GB // P
BN_EPS = 1e-5
ROOT = 1024.0
N_WARM = 5
WEAVE = 2
HEAT = 256
HEAT_U = 2
N_KEEP = 6
G_W = 7
CHUNK = 256
NCH = B // CHUNK
INV = 1.0 / CHUNK
NG = 3

FLOPS = 2 * B * K * C


def tile_binarymlp_pb_t_kernel(tc, z2, g2, beta2, W3, b3, out):
    nc = tc.nc
    with ExitStack() as ctx:
        const = ctx.enter_context(tc.tile_pool(name="const", bufs=1))
        big = ctx.enter_context(tc.tile_pool(name="big", bufs=8))
        st = ctx.enter_context(tc.tile_pool(name="st", bufs=4))
        zsp = ctx.enter_context(tc.tile_pool(name="zsp", bufs=3))
        grp = ctx.enter_context(tc.tile_pool(name="grp", bufs=3))
        cod = ctx.enter_context(tc.tile_pool(name="cod", bufs=3))
        small = ctx.enter_context(tc.tile_pool(name="small", bufs=4))
        psa = ctx.enter_context(tc.psum_pool(name="psa", bufs=4))
        pst = ctx.enter_context(tc.psum_pool(name="pst", bufs=4))
        ctx.enter_context(tc.manual_schedule())

        zns = []
        for g in range(G):
            zn = big.tile([P, J, K], BF16, tag="big", name="zn%d" % g, align_bytes=64)
            zns.append(zn)

        def load(u):
            g, h = divmod(u, 2)
            rows_u = z2[u * UB : (u + 1) * UB, :].rearrange("(p j) k -> p j k", j=JH)
            n = JH if u == 0 else 1
            for i in range(n):
                j0, j1 = i * JH // n, (i + 1) * JH // n
                nc.sync.dma_start(out=zns[g][:, h * JH + j0 : h * JH + j1, :], in_=rows_u[:, j0:j1, :])

        load(0)
        load(1)

        wcodes = const.tile([P, 2 * C], U32, name="wcodes", align_bytes=64)
        wscl = const.tile([P, 2 * C], U8, name="wscl", align_bytes=64)
        nc.vector.memset(wscl[:, 0:C].bitcast(I32), 0)
        nc.vector.memset(wcodes[:, 0:C].bitcast(I32), 0)
        brow = const.tile([P, C], BF16, name="brow")
        nc.vector.memset(brow[:], 0.0)
        vecs = const.tile([P, PASS_K], BF16, name="vecs")
        nc.vector.memset(vecs[:], 0.0)
        nc.scalar.dma_start(out=brow[0:1, :], in_=b3.rearrange("(o c) -> o c", o=1))
        nc.scalar.dma_start(out=vecs[0:2, :], in_=g2.rearrange("(c x) -> c x", x=PASS_K))
        nc.scalar.dma_start(out=vecs[2:4, :], in_=beta2.rearrange("(c x) -> c x", x=PASS_K))
        one = const.tile([P, 1], F32, name="one")
        nc.vector.memset(one[:], 1.0)
        warm = const.tile([P, 1], F32, name="warm")
        nc.scalar.activation(out=warm[:], in_=one[:], func=ACT.Sqrt)

        pwarm = psa.tile([P, C], F32, tag="acc", name="pwarm")
        for i in range(N_WARM):
            nc.tensor.matmul_mx(
                out=pwarm[:],
                lhsT=wcodes[:, 0:P].bitcast(FP8X4),
                lhsT_scale=wscl[:, 0:P],
                rhs=wcodes[:, 0:C].bitcast(FP8X4),
                rhs_scale=wscl[:, 0:C],
                start=True,
                stop=True,
            )

        ident = const.tile([P, P], BF16, name="ident")
        make_identity(nc, ident[:])
        identf = const.tile([P, P], F32, name="identf")
        make_identity(nc, identf[:])
        ones = const.tile([P, P], BF16, name="ones")
        nc.vector.memset(ones[:], 1.0)
        inv_col = const.tile([P, 1], BF16, name="inv_col")
        nc.vector.memset(inv_col[:], INV)
        pe_pos = const.tile([P, J], F32, name="pe_pos")
        nc.gpsimd.memset(pe_pos[:], 1.0 / ROOT)

        bs = const.tile([P, 2 * NCH * 6], F32, name="bs")
        msq = const.tile([P, 4 * NCH], F32, name="msq")
        qsum = const.tile([P, 2, 2 * NCH], F32, name="qsum")
        sq = const.tile([P, 2, U], F32, name="sq")
        ab = const.tile([P, 4 * P], F32, name="ab", align_bytes=64)
        nc.gpsimd.memset(ab[:], 0.0)
        rows = const.tile([P, PASS_K], F32, name="rows", align_bytes=64)
        nc.gpsimd.memset(rows[:], 0.0)
        stat = const.tile([P, 2 * KT], F32, name="stat")
        junk_s = const.tile([P, 2, 2, UB], BF16, name="junk_s")
        junk_e = const.tile([P, JH, C], BF16, name="junk_e")
        junk_d = const.tile([P, NG, P], F32, name="junk_d")
        gb = const.tile([P, 2 * KT], F32, name="gb")
        bias_bc = const.tile([P, C], F32, name="bias_bc")

        grams = []
        for i in range(NG):
            grams.append(psa.tile([P, P], F32, tag="acc", name="gram%d" % i))
        psums = psa.tile([P, C], F32, tag="acc", name="psums")
        plain = [(0, 0), (0, 1), (1, 0), (1, 1)]
        cols = [c * PASS_K + 256 + h * P for c, h in plain]

        gw = st.tile([P, 2, C, 4], BF16, tag="st", name="gw", align_bytes=64)

        def w_bank(n):
            c, ct = divmod(2 * n, C // P)
            ww = wn[:].bitcast(F32)
            pw = pst.tile([P, 2, 2, P], F32, tag="tr", name="pw")
            for i in range(2):
                for u in range(2):
                    nc.tensor.transpose(
                        pw[:, i, u, :], ww[:, ct + i, 256 * c + u : 256 * (c + 1) : 2], identf[:]
                    )
            for i in range(2):
                nc.scalar.copy(
                    out=gw[:, c, (ct + i) * P : (ct + i + 1) * P, :].bitcast(F32),
                    in_=pw[:, i, :, :].rearrange("p u n -> p n u"),
                )

        def small_vectors():
            pv = pst.tile([P, 4, P], BF16, tag="tr", name="pv")
            for t in range(4):
                nc.tensor.transpose(pv[:, t, :], vecs[:, t:PASS_K:4], ident[:])
            pb = pst.tile([P, C], F32, tag="tr", name="pb")
            nc.tensor.matmul(out=pb[:], lhsT=ones[:], rhs=brow[:], start=True, stop=True)
            nc.scalar.copy(out=bias_bc[:], in_=pb[:])
            return pv

        def word_tile(u, c, j):
            g, h = divmod(u, 2)
            return zns[g][:].bitcast(F32)[:, h * JH + j, 256 * c : 256 * c + P]

        def word_stats(u, c, pw2):
            pairs = pw2[:].bitcast(BF16)
            for q in range(2):
                n = (c * NCH + 2 * u + q) * 6
                nc.vector.bn_stats(out=bs[:, n : n + 6], in_=pairs[:, q * 512 : (q + 1) * 512])

        def heat(n):
            for i in range(n):
                nc.tensor.matmul_mx(
                    out=psums[:, C - HEAT : C],
                    lhsT=wcodes[:, 0:P].bitcast(FP8X4),
                    lhsT_scale=wscl[:, 0:P],
                    rhs=wcodes[:, 0:HEAT].bitcast(FP8X4),
                    rhs_scale=wscl[:, 0:HEAT],
                    start=True,
                    stop=True,
                )

        ahead = pst.tile([P, UB], F32, tag="tr", name="pw2")
        for j in range(JH):
            nc.tensor.transpose(ahead[:, j * P : (j + 1) * P], word_tile(0, 0, j), identf[:])
            heat(1)
        for u in range(U):
            g, h = divmod(u, 2)
            if h == 1 and g + 1 < G:
                load(u + 1)
                load(u + 2)
            if u == 2 * G_W:
                wn = st.tile([P, C // P, K], BF16, tag="st", name="wn", align_bytes=64)
                nc.sync.dma_start(out=wn[:], in_=W3.rearrange("(t p) k -> p t k", p=P))
            zn = zns[g]
            js = range(h * JH, (h + 1) * JH)
            squares = [(i, j) for i in range(NG) for j in js]
            sums = [(i, j) for i in range(NG) for j in js]

            def weave(n):
                for i, j in squares[n * WEAVE : (n + 1) * WEAVE]:
                    nc.tensor.matmul(
                        out=grams[i][:],
                        lhsT=zn[:, j, cols[i] : cols[i] + P],
                        rhs=zn[:, j, cols[i] : cols[i] + P],
                        start=(u == 0 and j == 0),
                        stop=(u == U - 1 and j == J - 1),
                    )
                for i, j in sums[n * WEAVE : (n + 1) * WEAVE]:
                    nc.tensor.matmul(
                        out=psums[:, i * U + u : i * U + u + 1],
                        lhsT=zn[:, j, cols[i] : cols[i] + P],
                        rhs=inv_col[:],
                        start=(j == js[0]),
                        stop=(j == js[-1]),
                    )

            first = ahead
            second = pst.tile([P, UB], F32, tag="tr", name="pw2")
            pt = pst.tile([P, UB], BF16, tag="tr", name="pt")
            if u + 1 < U:
                ahead = pst.tile([P, UB], F32, tag="tr", name="pw2")
            n_t = 0
            for kind in range(3):
                for j in range(JH):
                    cut = slice(j * P, (j + 1) * P)
                    if kind == 0:
                        nc.tensor.transpose(second[:, cut], word_tile(u, 1, j), identf[:])
                    elif kind == 1:
                        nc.tensor.transpose(pt[:, cut], zn[:, h * JH + j, cols[3] : cols[3] + P], ident[:])
                    elif u + 1 < U:
                        nc.tensor.transpose(ahead[:, cut], word_tile(u + 1, 0, j), identf[:])
                    n_t += 1
                    if n_t % WEAVE == 0:
                        weave(n_t // WEAVE - 1)
                        if u < HEAT_U and n_t % JH == 0:
                            heat(2)
            word_stats(u, 0, first)
            word_stats(u, 1, second)
            nc.scalar.activation(out=junk_s[:, h, 0, :], in_=pt[:], func=ACT.Square, accum_out=sq[:, 1, u : u + 1])
            nc.scalar.activation(
                out=junk_s[:, h, 1, :], in_=pt[:], func=ACT.Copy, scale=INV, accum_out=sq[:, 0, u : u + 1]
            )

        dts = {}
        wts = {}

        def late_tile(g, t, early=False):
            if early:
                dt = psa.tile([P, GB], BF16, tag="acc", name="dte")
            else:
                dt = pst.tile([P, GB], BF16, tag="tr", name="dt")
            dts[(g, t)] = dt
            for j in range(J):
                nc.tensor.transpose(dt[:, j * P : (j + 1) * P], zns[g][:, j, t:PASS_K:4], ident[:])

        def late_words(v, u):
            g, h = divmod(v, 2)
            wt = pst.tile([P, UB], F32, tag="tr", name="wt")
            wts[(v, u)] = wt
            zw = zns[g][:].bitcast(F32)
            for j in range(JH):
                nc.tensor.transpose(
                    wt[:, j * P : (j + 1) * P], zw[:, h * JH + j, 256 + u : 512 : 2], identf[:]
                )

        pv = small_vectors()
        w_bank(0)
        w_bank(1)

        abv = ab[:].rearrange("p (u h x) -> p u h x", u=2, h=2)
        bsv = bs[:].rearrange("p (n e f) -> p e n f", e=2, f=3)
        mean_v = bsv[:, :, :, 1]
        nc.vector.tensor_tensor(
            out=msq[:].rearrange("p (e n) -> p e n", e=2), in0=mean_v, in1=mean_v, op=ALU.mult
        )
        nc.vector.tensor_reduce(
            out=abv[:, 0, :, 0:2],
            in_=bs[:].rearrange("p (c n e f) -> p e c n f", c=2, e=2, f=3)[:, :, :, :, 1],
            axis=AX.X,
            op=ALU.add,
        )
        nc.vector.scalar_tensor_tensor(
            out=qsum[:],
            in0=msq[:].rearrange("p (e n) -> p e n", e=2),
            scalar=float(CHUNK),
            in1=bsv[:, :, :, 2],
            op0=ALU.mult,
            op1=ALU.add,
        )
        for i in range(NG):
            c, h = plain[i]
            nc.vector.scalar_tensor_tensor(
                out=junk_d[:, i, :],
                in0=grams[i][:],
                scalar=1.0,
                in1=ident[:],
                op0=ALU.mult,
                op1=ALU.mult,
                accum_out=abv[:, 1, h, 2 + c : 3 + c],
            )
        nc.vector.tensor_reduce(
            out=abv[:, 0, :, 2:4], in_=qsum[:].rearrange("p e (c n) -> p e c n", c=2), axis=AX.X, op=ALU.add
        )
        nc.vector.tensor_reduce(
            out=abv[:, 1, :, 0],
            in_=psums[:, 0 : 2 * U].rearrange("p (h u) -> p h u", h=2),
            axis=AX.X,
            op=ALU.add,
        )
        nc.vector.tensor_reduce(
            out=abv[:, 1, 0, 1:2], in_=psums[:, 2 * U : 3 * U], axis=AX.X, op=ALU.add
        )
        nc.vector.tensor_reduce(out=abv[:, 1, 1, 1:4:2], in_=sq[:], axis=AX.X, op=ALU.add)
        nc.vector.tensor_copy(
            out=gb[:].rearrange("p (r t) -> p r t", t=4), in_=pv[:, :, 0:4].rearrange("p t r -> p r t")
        )
        pt1 = psa.tile([P, 4 * P], F32, tag="acc", name="pt1")
        for q in range(4):
            nc.tensor.transpose(pt1[:, q * P : (q + 1) * P], ab[:, q * P : (q + 1) * P], identf[:])
        w_bank(2)
        rows_v = rows[0:4, :].rearrange("r (t p) -> r t p", t=4)
        for e in range(2):
            nc.vector.tensor_copy(
                out=rows_v[:, e:4:2, 0:64],
                in_=pt1[0:4, e * P : (e + 1) * P].rearrange("r (p d) -> r d p", d=2),
            )
        nc.vector.tensor_copy(
            out=rows_v[:, :, 64:P], in_=pt1[0:4, 256:512].rearrange("r (p t) -> r t p", t=4)
        )
        pt2 = psa.tile([P, 4, P], F32, tag="acc", name="pt2")
        for t in range(4):
            nc.tensor.transpose(pt2[:, t, :], rows[:, t * P : (t + 1) * P], identf[:])
        nc.vector.tensor_copy(
            out=stat[:].rearrange("p (r t) -> p r t", t=4), in_=pt2[:, :, 0:4].rearrange("p t r -> p r t")
        )
        late_tile(0, 0)
        w_bank(3)
        late_words(0, 0)
        late_tile(0, 1)
        late_words(0, 1)
        late_tile(0, 2, early=True)
        late_tile(0, 3, early=True)
        ssum = stat[:, 0:KT]
        ssq = stat[:, KT : 2 * KT]
        m2 = const.tile([P, KT], F32, name="m2")
        nc.vector.scalar_tensor_tensor(
            out=m2[:], in0=ssum, scalar=float(CHUNK * CHUNK) / (B * B), in1=ssum, op0=ALU.mult, op1=ALU.mult
        )
        var = const.tile([P, KT], F32, name="var")
        nc.vector.scalar_tensor_tensor(
            out=var[:], in0=ssq, scalar=1.0 / B, in1=m2[:], op0=ALU.mult, op1=ALU.subtract
        )
        ve = const.tile([P, KT], F32, name="ve")
        nc.vector.tensor_scalar(
            out=ve[:], in0=var[:], scalar1=0.0, scalar2=BN_EPS, op0=ALU.max, op1=ALU.add
        )
        sd = const.tile([P, KT], F32, name="sd")
        nc.scalar.activation(out=sd[:], in_=ve[:], func=ACT.Sqrt)
        nc.scalar.activation(out=warm[:], in_=one[:], func=ACT.Exp)
        mean = const.tile([P, KT], F32, name="mean")
        nc.vector.tensor_scalar(
            out=mean[:], in0=ssum, scalar1=float(CHUNK) / B, scalar2=None, op0=ALU.mult
        )
        rstd = const.tile([P, KT], F32, name="rstd")
        nc.vector.reciprocal(out=rstd[:], in_=sd[:])
        a = const.tile([P, KT], F32, name="a")
        nc.vector.tensor_tensor(out=a[:], in0=gb[:, 0:KT], in1=rstd[:], op=ALU.mult)
        ma = const.tile([P, KT], F32, name="ma")
        nc.vector.tensor_tensor(out=ma[:], in0=mean[:], in1=a[:], op=ALU.mult)
        bb = const.tile([P, KT], F32, name="bb")
        nc.vector.tensor_tensor(out=bb[:], in0=gb[:, KT : 2 * KT], in1=ma[:], op=ALU.subtract)

        ghs = {}
        cds = {}
        scs = {}
        accs = {}
        lts = {}
        negs = {}
        esums = {}
        rpos = {}
        rneg = {}
        lnt = {}
        lne = {}
        lnq = {}
        lnp = {}
        lnw = {}
        shifts = {}
        ztas = {}
        zss = {}

        def affine_v(g, t):
            if t == 0:
                ztas[g] = st.tile([P, 4, GB], BF16, tag="st", name="zta", align_bytes=64)
            nc.vector.tensor_scalar(
                out=ztas[g][:, t, :],
                in0=dts[(g, t)][:],
                scalar1=a[:, t : t + 1],
                scalar2=bb[:, t : t + 1],
                op0=ALU.mult,
                op1=ALU.add,
            )

        def affine_s(v):
            zss[v] = zsp.tile([P, 4, UB], BF16, tag="zs", name="zs", align_bytes=64)
            for u in range(2):
                pairs = wts[(v, u)][:].bitcast(BF16)
                for e in range(2):
                    kt = 4 + 2 * u + e
                    nc.scalar.activation(
                        out=zss[v][:, 2 * u + e, :],
                        in_=pairs[:, e : 2 * UB : 2],
                        func=ACT.Relu,
                        bias=bb[:, kt : kt + 1],
                        scale=a[:, kt : kt + 1],
                    )

        def regroup(v, c, b0, b1, engine):
            g, h = divmod(v, 2)
            if v not in ghs:
                ghs[v] = grp.tile([P, 2, UB, 4], BF16, tag="gr", name="gh", align_bytes=64)
            four = ztas[g][:, :, h * UB : (h + 1) * UB] if c == 0 else zss[v][:]
            dst = ghs[v][:, c, b0:b1, :].rearrange("p (n i) t -> p n t i", i=4)
            src = four[:, :, b0:b1].rearrange("p t (n i) -> p n t i", i=4)
            if engine == "V":
                nc.vector.tensor_scalar(out=dst, in0=src, scalar1=0.0, scalar2=None, op0=ALU.max)
            elif engine == "G":
                nc.gpsimd.tensor_scalar(
                    out=ghs[v][:, c, b0:b1, :],
                    in0=four[:, :, b0:b1].rearrange("p t n -> p n t"),
                    scalar1=1.0,
                    scalar2=0.0,
                    op0=ALU.mult,
                    op1=ALU.add,
                )
            else:
                nc.scalar.activation(out=dst, in_=src, func=ACT.Relu)

        def quant(v):
            cd = cod.tile([P, 2 * UB], U32, tag="cd", name="cd", align_bytes=64)
            sc = cod.tile([P, 2 * UB], U8, tag="sc", name="sc", align_bytes=64)
            cds[v] = cd
            scs[v] = sc
            nc.vector.quantize_mx(
                out=cd[:].bitcast(FP8X4),
                scales=sc[:],
                in_=ghs[v][:].rearrange("p c b t -> p (c b t)"),
            )

        def keep_warm(n):
            pk = psa.tile([P, C], F32, tag="acc", name="pk")
            for i in range(n):
                nc.tensor.matmul_mx(
                    out=pk[:],
                    lhsT=wcodes[:, 0:P].bitcast(FP8X4),
                    lhsT_scale=wscl[:, 0:P],
                    rhs=wcodes[:, 0:C].bitcast(FP8X4),
                    rhs_scale=wscl[:, 0:C],
                    start=True,
                    stop=True,
                )

        def mx(v, jj):
            acc = psa.tile([P, C], F32, tag="acc", name="acc")
            accs[(v, jj)] = acc
            for c in range(2):
                col = c * UB + jj * P
                nc.tensor.matmul_mx(
                    out=acc[:],
                    lhsT=cds[v][:, col : col + P].bitcast(FP8X4),
                    lhsT_scale=scs[v][:, col : col + P],
                    rhs=wcodes[:, c * C : (c + 1) * C].bitcast(FP8X4),
                    rhs_scale=wscl[:, c * C : (c + 1) * C],
                    start=(c == 0),
                    stop=(c == 1),
                )

        def add_bias(v, jj):
            g, h = divmod(v, 2)
            if h == 0 and jj == 0:
                lts[g] = big.tile([P, J, C], F32, tag="big", name="lt", align_bytes=64)
                negs[g] = small.tile([P, J], F32, name="neg_m")
                esums[g] = small.tile([P, J], F32, name="esum")
            nc.vector.tensor_tensor(
                out=lts[g][:, h * JH + jj, :], in0=accs[(v, jj)][:], in1=bias_bc[:], op=ALU.add
            )

        def row_max(v, jj0, jj1):
            g, h = divmod(v, 2)
            nc.vector.tensor_reduce(
                out=negs[g][:, h * JH + jj0 : h * JH + jj1],
                in_=lts[g][:, h * JH + jj0 : h * JH + jj1, :],
                axis=AX.X,
                op=ALU.max,
                negate=True,
            )

        def expsum(v, jj0=0, jj1=JH):
            g, h = divmod(v, 2)
            for jj in range(jj0, jj1):
                j = h * JH + jj
                nc.scalar.activation(
                    out=junk_e[:, jj, :],
                    in_=lts[g][:, j, :],
                    func=ACT.Exp,
                    bias=negs[g][:, j : j + 1],
                    scale=1.0,
                    accum_out=esums[g][:, j : j + 1],
                )

        def ln_pow(key):
            g, j0, j1 = key
            rpos[key] = small.tile([P, J], F32, name="r_pos")
            nc.gpsimd.tensor_tensor(
                out=rpos[key][:, j0:j1], in0=esums[g][:, j0:j1], in1=pe_pos[:, j0:j1], op=ALU.pow
            )

        def ln_recip(key):
            g, j0, j1 = key
            rneg[key] = small.tile([P, J], F32, name="r_neg")
            nc.vector.reciprocal(out=rneg[key][:, j0:j1], in_=rpos[key][:, j0:j1])

        def ln_diff(key):
            g, j0, j1 = key
            lnt[key] = small.tile([P, J], F32, name="t")
            nc.gpsimd.tensor_tensor(
                out=lnt[key][:, j0:j1], in0=rpos[key][:, j0:j1], in1=rneg[key][:, j0:j1], op=ALU.subtract
            )

        def ln_exp(key):
            g, j0, j1 = key
            lne[key] = small.tile([P, J], F32, name="e")
            nc.scalar.activation(
                out=lne[key][:, j0:j1], in_=lnt[key][:, j0:j1], func=ACT.Exp, scale=-0.5 * ROOT
            )

        def ln_first(key):
            g, j0, j1 = key
            lnq[key] = small.tile([P, J], F32, name="q")
            nc.gpsimd.tensor_scalar(
                out=lnq[key][:, j0:j1],
                in0=lnt[key][:, j0:j1],
                scalar1=-0.5 * ROOT,
                scalar2=1.0,
                op0=ALU.mult,
                op1=ALU.add,
            )

        def ln_second(key):
            g, j0, j1 = key
            lnp[key] = small.tile([P, J], F32, name="q2")
            nc.gpsimd.tensor_tensor(
                out=lnp[key][:, j0:j1], in0=lnq[key][:, j0:j1], in1=negs[g][:, j0:j1], op=ALU.add
            )

        def ln_mul(key):
            g, j0, j1 = key
            lnw[key] = small.tile([P, J], F32, name="w")
            nc.gpsimd.tensor_tensor(
                out=lnw[key][:, j0:j1], in0=esums[g][:, j0:j1], in1=lne[key][:, j0:j1], op=ALU.mult
            )

        def ln_shift(key):
            g, j0, j1 = key
            neg_c = small.tile([P, J], F32, name="neg_c")
            nc.gpsimd.tensor_tensor(
                out=neg_c[:, j0:j1], in0=lnp[key][:, j0:j1], in1=lnw[key][:, j0:j1], op=ALU.subtract
            )
            for j in range(j0, j1):
                shifts[(g, j)] = neg_c[:, j : j + 1]

        def ln_table(key):
            g, j0, j1 = key
            y = small.tile([P, J], F32, name="y")
            lne[key] = y
            nc.scalar.activation(out=y[:, j0:j1], in_=esums[g][:, j0:j1], func=ACT.Ln)

        def ln_table_shift(key):
            g, j0, j1 = key
            neg_c = small.tile([P, J], F32, name="neg_c")
            nc.vector.tensor_tensor(
                out=neg_c[:, j0:j1], in0=negs[g][:, j0:j1], in1=lne[key][:, j0:j1], op=ALU.subtract
            )
            for j in range(j0, j1):
                shifts[(g, j)] = neg_c[:, j : j + 1]

        def subtract(v, engines, between=()):
            g, h = divmod(v, 2)
            lt = lts[g]
            for jj in range(JH):
                j = h * JH + jj
                shift = shifts[(g, j)]
                engine = engines[jj]
                if engine == "V":
                    nc.vector.tensor_scalar(
                        out=lt[:, j, :], in0=lt[:, j, :], scalar1=shift, scalar2=None, op0=ALU.add
                    )
                elif engine == "G":
                    nc.gpsimd.tensor_scalar(
                        out=lt[:, j, :], in0=lt[:, j, :], scalar1=1.0, scalar2=shift, op0=ALU.mult, op1=ALU.add
                    )
                elif engine == "S":
                    nc.scalar.activation(
                        out=lt[:, j, :], in_=lt[:, j, :], func=ACT.Identity, bias=shift, scale=1.0
                    )
                if jj < len(between):
                    between[jj]()

        def store(v):
            g, h = divmod(v, 2)
            nc.sync.dma_start(
                out=out[v * UB : (v + 1) * UB, :].rearrange("(p j) c -> p j c", j=JH),
                in_=lts[g][:, h * JH : (h + 1) * JH, :],
            )

        def subtract_store(v, engines):
            subtract(v, engines)
            store(v)

        affine_s(0)
        for t in range(4):
            affine_v(0, t)
            if t < 2:
                late_words(1, t)
            else:
                late_tile(1, t - 2)
            if t == 1:
                nc.vector.quantize_mx(
                    out=wcodes[:].bitcast(FP8X4),
                    scales=wscl[:],
                    in_=gw[:].rearrange("p c n t -> p (c n t)"),
                )
        regroup(0, 0, 0, UB, "V")
        affine_s(1)
        late_tile(1, 2)
        late_tile(1, 3)
        for n in range(0, UB - P, P):
            regroup(0, 1, n, n + P, "G")
        for t in range(2):
            affine_v(1, t)
            late_words(2, t)
        regroup(0, 1, UB - P, UB, "V")
        quant(0)
        for n in range(0, UB // 2, P):
            regroup(1, 1, n, n + P, "G")
        keep_warm(N_KEEP)
        for jj in range(JH):
            mx(0, jj)
        for t in range(2, 4):
            affine_v(1, t)
            late_tile(2, t - 2)
        regroup(1, 1, UB // 2, UB, "V")
        regroup(1, 0, 0, UB, "S")
        affine_s(2)
        late_words(3, 0)
        late_words(3, 1)
        quant(1)
        for v in range(U - 2):
            g_a, t_a = (v + 4) // 2, 2 * (v % 2)
            g_t, t_t = (v + 5) // 2, 2 * ((v + 1) % 2)
            key_p = ((v - 3) // 2, 0, J)
            key_l = ((v - 4) // 2, 0, J)
            key_s = ((v - 5) // 2, 0, J)
            odd = v % 2 == 1
            if odd and v >= 5:
                ln_mul(key_s)
            regroup(v + 2, 0, 0, UB, "S")
            regroup(v + 2, 1, 0, UB, "G")
            if odd and v >= 5:
                ln_shift(key_s)
            if odd and v >= 3:
                ln_pow(key_p)
            if not odd and v >= 4:
                ln_diff(key_l)
            if v + 3 < U:
                affine_s(v + 3)
            if not odd and v >= 4:
                ln_exp(key_l)
            for jj in range(JH):
                add_bias(v, jj)
                mx(v + 1, jj)
                if jj > 0:
                    row_max(v, jj - 1, jj)
                elif v >= 1:
                    row_max(v - 1, JH - 1, JH)
                if jj < 2:
                    if g_a < G:
                        affine_v(g_a, t_a + jj)
                    if g_t < G:
                        late_tile(g_t, t_t + jj)
                elif v + 4 < U:
                    late_words(v + 4, jj - 2)
                if jj == 2:
                    quant(v + 2)
                    if v >= 5:
                        subtract(v - 5, "-V-V")
            if odd and v >= 3:
                ln_recip(key_p)
            if v >= 1:
                expsum(v - 1)
            if v >= 5:
                between = () if odd or v < 4 else (lambda: ln_first(key_l), lambda: None, lambda: ln_second(key_l))
                subtract(v - 5, "G-G-", between)
                store(v - 5)
            if v == U - 3:
                subtract_store(v - 4, "SSSS")
            elif v == 4:
                ln_first(key_l)
                ln_second(key_l)
        key_a = (G - 3, 0, J)
        key_b = (G - 2, 0, J)
        key_c = (G - 1, 0, JH)
        row_max(U - 3, JH - 1, JH)
        ln_diff(key_a)
        ln_exp(key_a)
        ln_first(key_a)
        ln_second(key_a)
        ln_mul(key_a)
        ln_shift(key_a)
        expsum(U - 3)
        subtract(U - 6, "GG--")
        ln_pow(key_b)
        subtract(U - 6, "--GG")
        store(U - 6)
        subtract_store(U - 5, "SSSS")
        for jj in range(JH):
            add_bias(U - 2, jj)
            mx(U - 1, jj)
            if jj > 0:
                row_max(U - 2, jj - 1, jj)
        row_max(U - 2, JH - 1, JH)
        ln_recip(key_b)
        ln_diff(key_b)
        ln_exp(key_b)
        ln_first(key_b)
        ln_second(key_b)
        ln_mul(key_b)
        ln_shift(key_b)
        expsum(U - 2)
        subtract(U - 4, "GG--")
        ln_pow(key_c)
        for jj in range(JH):
            add_bias(U - 1, jj)
            if jj > 0:
                row_max(U - 1, jj - 1, jj)
        row_max(U - 1, JH - 1, JH)
        ln_recip(key_c)
        subtract(U - 4, "--GV")
        store(U - 4)
        ln_diff(key_c)
        expsum(U - 1, 0, 3)
        ln_exp(key_c)
        expsum(U - 1, 3, JH)
        ln_first(key_c)
        ln_second(key_c)
        ln_mul(key_c)
        ln_shift(key_c)
        last = (G - 1, JH, J)
        ln_table(last)
        subtract_store(U - 3, "VVVV")
        subtract_store(U - 2, "GVVG")
        ln_table_shift(last)
        subtract_store(U - 1, "VSSV")
